import numpy as np
import ml_dtypes


def mxq(x, axis, fmt="e4m3"):
    dtype, down = {"e4m3": (ml_dtypes.float8_e4m3fn, 7), "e5m2": (ml_dtypes.float8_e5m2, 14)}[fmt]
    v = np.moveaxis(np.asarray(x, np.float32).astype(ml_dtypes.bfloat16).astype(np.float64), axis, -1)
    blocks = v.reshape(v.shape[:-1] + (-1, 32))
    amax = np.abs(blocks).max(-1, keepdims=True)
    byte = np.maximum(np.where(amax > 0, np.frexp(amax)[1] - 1 + 127, 0) - down, 1)
    scale = np.exp2(byte - 127.0)
    codes = (blocks / scale).astype(np.float32).astype(dtype).astype(np.float64)
    return np.moveaxis((codes * scale).reshape(v.shape), -1, axis)


WIDE = False


def mx_kscale(k):
    if not WIDE:
        return np.ones(k)
    levels = np.array([10, -10, 5, -5, 0])
    if k % 512:
        return np.exp2(np.random.permutation(np.resize(levels, k // 32))).repeat(32)
    a = np.empty((k // 512, 16))
    for p in range(k // 512):
        a[p, :8] = np.random.permutation(np.resize(levels, 8))
        for g in range(8):
            far = levels[np.abs(levels - a[p, g]) >= 10]
            a[p, g + 8] = far[np.random.randint(len(far))]
    return np.exp2(a.ravel()).repeat(32)


BF16 = ml_dtypes.bfloat16


def bf(x):
    return np.asarray(x, np.float32).astype(BF16)


def f64(x):
    return np.asarray(x).astype(np.float64)


B, S, HID, H, KV, D = 1, 4096, 1024, 2, 1, 128
EPS = 1e-6
THETA = 10000.0
HALF = D // 2


def rotate_half(x):
    return np.concatenate([-x[..., HALF:], x[..., :HALF]], axis=-1)


def rms_norm(x, w=None):
    n = x * (1.0 / np.sqrt(np.mean(x * x, axis=-1, keepdims=True) + EPS))
    return n if w is None else n * w


def setup_inputs():
    s = mx_kscale(HID)
    c = 0.004 / np.sqrt(HID)
    inv_freq = 1.0 / THETA ** (np.arange(0, D, 2) / D)
    pos = np.random.randint(0, S) + np.arange(S)
    freqs = pos[:, None] * inv_freq[None, :]
    emb = np.concatenate([freqs, freqs], axis=-1)
    return {"hidden_states": bf(np.random.standard_normal((B, S, HID)) * s),
            "cos": bf(np.cos(emb)[None]),
            "sin": bf(np.sin(emb)[None]),
            "Wq": bf(np.random.standard_normal((H * D, HID)) * c / s[None, :]),
            "Wk": bf(np.random.standard_normal((KV * D, HID)) * c / s[None, :]),
            "Wv": bf(np.random.standard_normal((KV * D, HID)) * c / s[None, :]),
            "q_norm_w": bf(0.5 + 0.1 * np.random.standard_normal(D)),
            "k_norm_w": bf(0.5 + 0.1 * np.random.standard_normal(D))}


def reference(hidden_states, cos, sin, Wq, Wk, Wv, q_norm_w, k_norm_w):
    xq = mxq(f64(hidden_states), 2, "e4m3")
    cs = f64(cos)[:, :, None, :]
    sn = f64(sin)[:, :, None, :]
    q = (xq @ mxq(f64(Wq).T, 0, "e4m3")).reshape(B, S, H, D)
    k = (xq @ mxq(f64(Wk).T, 0, "e4m3")).reshape(B, S, KV, D)
    v = (xq @ mxq(f64(Wv).T, 0, "e4m3")).reshape(B, S, KV, D)
    q = rms_norm(q, f64(q_norm_w))
    q = q * cs + rotate_half(q) * sn
    k = rms_norm(k, f64(k_norm_w))
    k = k * cs + rotate_half(k) * sn
    v = rms_norm(v)
    return q.transpose(0, 2, 1, 3), k.transpose(0, 2, 1, 3), v.transpose(0, 2, 1, 3)

@@ -1,0 +1,268 @@
+from contextlib import ExitStack
+
+import concourse.mybir as mybir
+from concourse.masks import make_identity
+
+BF16 = mybir.dt.bfloat16
+F32 = mybir.dt.float32
+U32 = mybir.dt.uint32
+U8 = mybir.dt.uint8
+FP8X4 = mybir.dt.float8_e4m3fn_x4
+ACT = mybir.ActivationFunctionType
+ALU = mybir.AluOpType
+
+P = 128
+PACK = 4
+K_PASS = P * PACK
+
+TOKENS = 4096
+HID = 1024
+D = 128
+HALF = D // 2
+EPS = 1e-6
+HEADS = 4
+ROTATED = 3
+V_HEAD = 3
+FEATURES = HEADS * D
+
+PASSES = HID // K_PASS
+WORDS = HID // 2
+TURNS = WORDS // P
+TILES = TOKENS // P
+TILES_PER_ROUND = 2
+ROUNDS = TILES // TILES_PER_ROUND
+LOAD_AHEAD = 6
+
+FLOPS = 2 * TOKENS * HID * FEATURES
+
+
+def tile_refattention_pa_t_kernel(
+    tc, hidden_states, cos, sin, Wq, Wk, Wv, q_norm_w, k_norm_w, out_0, out_1, out_2
+):
+    nc = tc.nc
+
+    x_view = hidden_states.flatten_outer_dims().rearrange("(p j) k -> p j k", j=TILES)
+    cos_view = cos.flatten_outer_dims().rearrange("(p j) d -> p j d", j=TILES)
+    sin_view = sin.flatten_outer_dims().rearrange("(p j) d -> p j d", j=TILES)
+    q_view = out_0.flatten_outer_dims().rearrange("(h p j) d -> p h j d", h=2, j=TILES)
+    k_view = out_1.flatten_outer_dims().rearrange("(p j) d -> p j d", j=TILES)
+    v_view = out_2.flatten_outer_dims().rearrange("(p j) d -> p j d", j=TILES)
+
+    with ExitStack() as stack:
+        stack.enter_context(tc.manual_schedule())
+        consts = stack.enter_context(tc.tile_pool(name="consts", bufs=1))
+        x_pool = stack.enter_context(tc.tile_pool(name="x", bufs=ROUNDS))
+        stage = stack.enter_context(tc.tile_pool(name="stage", bufs=2))
+        stats = stack.enter_context(tc.tile_pool(name="stats", bufs=3))
+        ring = stack.enter_context(tc.tile_pool(name="ring", bufs=3))
+        results = stack.enter_context(tc.tile_pool(name="results", bufs=4))
+        psum_turn = stack.enter_context(tc.psum_pool(name="psum_turn", bufs=2 * TILES_PER_ROUND))
+        psum_prod = stack.enter_context(tc.psum_pool(name="psum_prod", bufs=2 * TILES_PER_ROUND))
+
+        gains = consts.tile([P, ROTATED, D], BF16)
+        nc.scalar.dma_start(out=gains[:, 0, :], in_=q_norm_w.partition_broadcast(P))
+        nc.scalar.dma_start(out=gains[:, 2, :], in_=k_norm_w.partition_broadcast(P))
+
+        w_raw = consts.tile([P, HEADS, HID], BF16)
+        for h, rows in enumerate((Wq[0:D, :], Wq[D : 2 * D, :], Wk, Wv)):
+            nc.sync.dma_start(out=w_raw[:, h, :], in_=rows)
+
+        x_of = {}
+
+        def load_tokens(r):
+            x_sb = x_pool.tile([P, TILES_PER_ROUND, HID], BF16)
+            first = r * TILES_PER_ROUND
+            nc.sync.dma_start(out=x_sb[:], in_=x_view[:, first : first + TILES_PER_ROUND, :])
+            x_of[r] = x_sb
+
+        cos_sb = consts.tile([P, TILES, D], BF16)
+        sin_sb = consts.tile([P, TILES, D], BF16)
+        load_tokens(0)
+        load_tokens(1)
+        nc.sync.dma_start(out=cos_sb[:], in_=cos_view)
+        nc.sync.dma_start(out=sin_sb[:], in_=sin_view)
+        load_tokens(2)
+
+        identity = consts.tile([P, P], F32)
+        make_identity(nc, identity[:])
+        eps = consts.tile([P, 1], F32)
+        nc.vector.memset(eps[:], EPS)
+        nc.vector.tensor_copy(out=gains[:, 1, :], in_=gains[:, 0, :])
+        table_warmer = consts.tile([P, 1], F32)
+        nc.scalar.activation(out=table_warmer[:], in_=eps[:], func=ACT.Abs_reciprocal_sqrt)
+
+        def turn(rows_as_words):
+            turned = psum_turn.tile([P, TURNS, P], F32)
+            for c in range(TURNS):
+                g, u = divmod(c, 2)
+                every_second = rows_as_words[:, 2 * P * g + u : 2 * P * (g + 1) : 2]
+                nc.tensor.transpose(turned[:, c, :], every_second, identity[:])
+            return turned
+
+        def side_by_side(turned):
+            return turned[:].rearrange("p (g u) r -> p g r u", u=2)
+
+        w_grouped = consts.tile([P, PASSES, FEATURES, PACK], BF16, align_bytes=64)
+        w_grouped_words = w_grouped[:].bitcast(F32)
+        w_words = w_raw[:].bitcast(F32)
+        for h in range(HEADS):
+            turned = turn(w_words[:, h, :])
+            copy_out = nc.scalar.copy if h % 2 == 0 else nc.vector.tensor_copy
+            copy_out(out=w_grouped_words[:, :, h * D : (h + 1) * D, :], in_=side_by_side(turned))
+        w_codes = consts.tile([P, PASSES, FEATURES], U32, align_bytes=64)
+        w_scales = consts.tile([P, PASSES, FEATURES], U8, align_bytes=64)
+        for g in range(PASSES):
+            nc.vector.quantize_mx(
+                out=w_codes[:, g, :].bitcast(FP8X4),
+                scales=w_scales[:, g, :],
+                in_=w_grouped[:, g, :, :].rearrange("p f t -> p (f t)"),
+            )
+
+        turned_of = {}
+        grouped_of = {}
+        codes_of = {}
+        product_of = {}
+        gained_of = {}
+        result_of = {}
+        normed_of = {}
+
+        def transpose_tokens(r):
+            x_words = x_of[r][:].bitcast(F32)
+            turned_of[r] = [turn(x_words[:, t, :]) for t in range(TILES_PER_ROUND)]
+
+        def regroup(r):
+            grouped = stage.tile([P, TILES_PER_ROUND, PASSES, P, PACK], BF16, align_bytes=64)
+            grouped_words = grouped[:].bitcast(F32)
+            for t in range(TILES_PER_ROUND):
+                nc.scalar.copy(out=grouped_words[:, t], in_=side_by_side(turned_of[r][t]))
+            grouped_of[r] = grouped
+
+        def quantise(r):
+            codes = stats.tile([P, TILES_PER_ROUND, PASSES, P], U32, align_bytes=64)
+            scales = stats.tile([P, TILES_PER_ROUND, PASSES, P], U8, align_bytes=64)
+            nc.vector.quantize_mx(
+                out=codes[:].rearrange("p t g r -> p (t g r)").bitcast(FP8X4),
+                scales=scales[:].rearrange("p t g r -> p (t g r)"),
+                in_=grouped_of[r][:].rearrange("p t g r v -> p (t g r v)"),
+            )
+            codes_of[r] = (codes, scales)
+
+        def project(r):
+            codes, scales = codes_of[r]
+            product_of[r] = []
+            for t in range(TILES_PER_ROUND):
+                product = psum_prod.tile([P, FEATURES], F32)
+                for g in range(PASSES):
+                    nc.tensor.matmul_mx(
+                        out=product[:],
+                        lhsT=codes[:, t, g, :].bitcast(FP8X4),
+                        lhsT_scale=scales[:, t, g, :],
+                        rhs=w_codes[:, g, :].bitcast(FP8X4),
+                        rhs_scale=w_scales[:, g, :],
+                        start=(g == 0),
+                        stop=(g == PASSES - 1),
+                    )
+                product_of[r].append(product)
+
+        def normalise(r):
+            sum_sq = stats.tile([P, TILES_PER_ROUND, HEADS], F32)
+            rstd = stats.tile([P, TILES_PER_ROUND, HEADS], F32)
+            squares = stage.tile([P, TILES_PER_ROUND, HEADS, D], BF16)
+            normed = ring.tile([P, ROTATED, TILES_PER_ROUND, D], F32)
+            result = results.tile([P, HEADS, TILES_PER_ROUND, D], F32)
+
+            def sum_squares(t, h):
+                nc.scalar.activation(
+                    out=squares[:, t, h, :],
+                    in_=product_of[r][t][:, h * D : (h + 1) * D],
+                    func=ACT.Square,
+                    accum_out=sum_sq[:, t, h : h + 1],
+                )
+
+            def reciprocal_rms(t):
+                nc.scalar.activation(
+                    out=rstd[:, t, :], in_=sum_sq[:, t, :], func=ACT.Abs_reciprocal_sqrt, scale=1.0 / D, bias=eps[:]
+                )
+
+            def times_rstd(t, h):
+                nc.scalar.activation(
+                    out=result[:, V_HEAD, t, :] if h == V_HEAD else normed[:, h, t, :],
+                    in_=product_of[r][t][:, h * D : (h + 1) * D],
+                    func=ACT.Copy,
+                    scale=rstd[:, t, h : h + 1],
+                )
+
+            every = [(t, h) for t in range(TILES_PER_ROUND) for h in range(HEADS)]
+            for t, h in every[:-2]:
+                sum_squares(t, h)
+            reciprocal_rms(0)
+            for t, h in every[-2:]:
+                sum_squares(t, h)
+            for t, h in every[: HEADS - 1]:
+                times_rstd(t, h)
+            reciprocal_rms(1)
+            for t, h in every[HEADS - 1 :]:
+                times_rstd(t, h)
+            normed_of[r] = normed
+            result_of[r] = result
+
+        def apply_gains(r):
+            gained = stage.tile([P, ROTATED, TILES_PER_ROUND, D], F32)
+            nc.vector.tensor_tensor(
+                out=gained[:],
+                in0=normed_of[r][:],
+                in1=gains[:].unsqueeze(2).to_broadcast([P, ROTATED, TILES_PER_ROUND, D]),
+                op=ALU.mult,
+            )
+            gained_of[r] = gained
+
+        def rotate_and_store(r):
+            first = r * TILES_PER_ROUND
+            tiles = slice(first, first + TILES_PER_ROUND)
+            low = slice(0, HALF)
+            high = slice(HALF, D)
+            result = result_of[r]
+
+            def over_heads(table, columns, width):
+                return table[:, tiles, columns].unsqueeze(1).to_broadcast([P, ROTATED, TILES_PER_ROUND, width])
+
+            gained = gained_of[r]
+            with_cos = stage.tile([P, ROTATED, TILES_PER_ROUND, D], F32)
+            with_sin = stage.tile([P, ROTATED, TILES_PER_ROUND, D], F32)
+            nc.vector.tensor_tensor(out=with_cos[:], in0=gained[:], in1=over_heads(cos_sb, slice(0, D), D), op=ALU.mult)
+            nc.vector.tensor_tensor(
+                out=with_sin[:, :, :, low], in0=gained[:, :, :, high], in1=over_heads(sin_sb, low, HALF), op=ALU.mult
+            )
+            nc.vector.tensor_tensor(
+                out=with_sin[:, :, :, high], in0=gained[:, :, :, low], in1=over_heads(sin_sb, high, HALF), op=ALU.mult
+            )
+            nc.vector.tensor_tensor(
+                out=result[:, 0:ROTATED, :, low], in0=with_cos[:, :, :, low], in1=with_sin[:, :, :, low], op=ALU.subtract
+            )
+            nc.vector.tensor_tensor(
+                out=result[:, 0:ROTATED, :, high], in0=with_cos[:, :, :, high], in1=with_sin[:, :, :, high], op=ALU.add
+            )
+            nc.sync.dma_start(out=q_view[:, :, tiles, :], in_=result[:, 0:2, :, :])
+            nc.sync.dma_start(out=k_view[:, tiles, :], in_=result[:, 2, :, :])
+            nc.sync.dma_start(out=v_view[:, tiles, :], in_=result[:, V_HEAD, :, :])
+
+        def in_range(r):
+            return 0 <= r < ROUNDS
+
+        for i in range(-3, ROUNDS):
+            if in_range(i + LOAD_AHEAD):
+                load_tokens(i + LOAD_AHEAD)
+            if in_range(i + 1):
+                project(i + 1)
+            if in_range(i + 3):
+                transpose_tokens(i + 3)
+            if in_range(i + 2):
+                regroup(i + 2)
+            if in_range(i + 1):
+                normalise(i + 1)
+            if in_range(i):
+                apply_gains(i)
+            if in_range(i + 2):
+                quantise(i + 2)
+            if in_range(i):
+                rotate_and_store(i)

@@ -32,6 +32,7 @@ TILES = TOKENS // P
 TILES_PER_ROUND = 2
 ROUNDS = TILES // TILES_PER_ROUND
 LOAD_AHEAD = 6
+TABLE_SPLIT = 4 * TILES_PER_ROUND
 
 FLOPS = 2 * TOKENS * HID * FEATURES
 
@@ -59,9 +60,10 @@ def tile_refattention_pa_t_kernel(
         psum_turn = stack.enter_context(tc.psum_pool(name="psum_turn", bufs=2 * TILES_PER_ROUND))
         psum_prod = stack.enter_context(tc.psum_pool(name="psum_prod", bufs=2 * TILES_PER_ROUND))
 
-        gains = consts.tile([P, ROTATED, D], BF16)
-        nc.scalar.dma_start(out=gains[:, 0, :], in_=q_norm_w.partition_broadcast(P))
-        nc.scalar.dma_start(out=gains[:, 2, :], in_=k_norm_w.partition_broadcast(P))
+        gain_rows = consts.tile([P, 2, D], BF16)
+        nc.vector.memset(gain_rows[:], 0.0)
+        for a, w in enumerate((q_norm_w, k_norm_w)):
+            nc.scalar.dma_start(out=gain_rows[0:1, a, :], in_=w.rearrange("(o d) -> o d", o=1))
 
         w_raw = consts.tile([P, HEADS, HID], BF16)
         for h, rows in enumerate((Wq[0:D, :], Wq[D : 2 * D, :], Wk, Wv)):
@@ -72,22 +74,29 @@ def tile_refattention_pa_t_kernel(
         def load_tokens(r):
             x_sb = x_pool.tile([P, TILES_PER_ROUND, HID], BF16)
             first = r * TILES_PER_ROUND
-            nc.sync.dma_start(out=x_sb[:], in_=x_view[:, first : first + TILES_PER_ROUND, :])
+            step = 1 if r == 0 else TILES_PER_ROUND
+            for t in range(0, TILES_PER_ROUND, step):
+                nc.sync.dma_start(out=x_sb[:, t : t + step, :], in_=x_view[:, first + t : first + t + step, :])
             x_of[r] = x_sb
 
         cos_sb = consts.tile([P, TILES, D], BF16)
         sin_sb = consts.tile([P, TILES, D], BF16)
+
+        def load_tables(first, last):
+            nc.sync.dma_start(out=cos_sb[:, first:last, :], in_=cos_view[:, first:last, :])
+            nc.sync.dma_start(out=sin_sb[:, first:last, :], in_=sin_view[:, first:last, :])
+
         load_tokens(0)
         load_tokens(1)
-        nc.sync.dma_start(out=cos_sb[:], in_=cos_view)
-        nc.sync.dma_start(out=sin_sb[:], in_=sin_view)
+        load_tables(0, TABLE_SPLIT)
         load_tokens(2)
 
         identity = consts.tile([P, P], F32)
         make_identity(nc, identity[:])
         eps = consts.tile([P, 1], F32)
         nc.vector.memset(eps[:], EPS)
-        nc.vector.tensor_copy(out=gains[:, 1, :], in_=gains[:, 0, :])
+        ones = consts.tile([P, P], BF16)
+        nc.vector.memset(ones[:], 1.0)
         table_warmer = consts.tile([P, 1], F32)
         nc.scalar.activation(out=table_warmer[:], in_=eps[:], func=ACT.Abs_reciprocal_sqrt)
 
@@ -105,18 +114,44 @@ def tile_refattention_pa_t_kernel(
         w_grouped = consts.tile([P, PASSES, FEATURES, PACK], BF16, align_bytes=64)
         w_grouped_words = w_grouped[:].bitcast(F32)
         w_words = w_raw[:].bitcast(F32)
-        for h in range(HEADS):
+        w_codes = consts.tile([P, PASSES, FEATURES], U32, align_bytes=64)
+        w_scales = consts.tile([P, PASSES, FEATURES], U8, align_bytes=64)
+
+        def prepare_head(h):
             turned = turn(w_words[:, h, :])
             copy_out = nc.scalar.copy if h % 2 == 0 else nc.vector.tensor_copy
             copy_out(out=w_grouped_words[:, :, h * D : (h + 1) * D, :], in_=side_by_side(turned))
-        w_codes = consts.tile([P, PASSES, FEATURES], U32, align_bytes=64)
-        w_scales = consts.tile([P, PASSES, FEATURES], U8, align_bytes=64)
-        for g in range(PASSES):
-            nc.vector.quantize_mx(
-                out=w_codes[:, g, :].bitcast(FP8X4),
-                scales=w_scales[:, g, :],
-                in_=w_grouped[:, g, :, :].rearrange("p f t -> p (f t)"),
-            )
+
+        def quantise_head(h):
+            columns = slice(h * D, (h + 1) * D)
+            for g in range(PASSES):
+                nc.vector.quantize_mx(
+                    out=w_codes[:, g, columns].bitcast(FP8X4),
+                    scales=w_scales[:, g, columns],
+                    in_=w_grouped[:, g, columns, :].rearrange("p f t -> p (f t)"),
+                )
+
+        prepare_head(0)
+        prepare_head(1)
+        quantise_head(0)
+        prepare_head(2)
+        prepare_head(3)
+        for h in range(1, HEADS):
+            quantise_head(h)
+
+        gains = consts.tile([P, ROTATED, D], BF16)
+        spread = psum_prod.tile([P, FEATURES], F32, tag="product")
+        nc.tensor.matmul(
+            out=spread[:, 0 : 2 * D],
+            lhsT=ones[:],
+            rhs=gain_rows[:].rearrange("p a d -> p (a d)"),
+            start=True,
+            stop=True,
+        )
+        nc.vector.tensor_copy(
+            out=gains[:, 0:2, :], in_=spread[:, 0:D].unsqueeze(1).to_broadcast([P, 2, D])
+        )
+        nc.vector.tensor_copy(out=gains[:, 2, :], in_=spread[:, D : 2 * D])
 
         turned_of = {}
         grouped_of = {}
@@ -134,7 +169,8 @@ def tile_refattention_pa_t_kernel(
             grouped = stage.tile([P, TILES_PER_ROUND, PASSES, P, PACK], BF16, align_bytes=64)
             grouped_words = grouped[:].bitcast(F32)
             for t in range(TILES_PER_ROUND):
-                nc.scalar.copy(out=grouped_words[:, t], in_=side_by_side(turned_of[r][t]))
+                copy_out = nc.vector.tensor_copy if r == 0 and t == 0 else nc.scalar.copy
+                copy_out(out=grouped_words[:, t], in_=side_by_side(turned_of[r][t]))
             grouped_of[r] = grouped
 
         def quantise(r):
@@ -151,7 +187,7 @@ def tile_refattention_pa_t_kernel(
             codes, scales = codes_of[r]
             product_of[r] = []
             for t in range(TILES_PER_ROUND):
-                product = psum_prod.tile([P, FEATURES], F32)
+                product = psum_prod.tile([P, FEATURES], F32, tag="product")
                 for g in range(PASSES):
                     nc.tensor.matmul_mx(
                         out=product[:],
@@ -252,6 +288,8 @@ def tile_refattention_pa_t_kernel(
         for i in range(-3, ROUNDS):
             if in_range(i + LOAD_AHEAD):
                 load_tokens(i + LOAD_AHEAD)
+            if i == -2:
+                load_tables(TABLE_SPLIT, TILES)
             if in_range(i + 1):
                 project(i + 1)
             if in_range(i + 3):

@@ -53,12 +53,13 @@ def tile_refattention_pa_t_kernel(
         stack.enter_context(tc.manual_schedule())
         consts = stack.enter_context(tc.tile_pool(name="consts", bufs=1))
         x_pool = stack.enter_context(tc.tile_pool(name="x", bufs=ROUNDS))
+        w_pool = stack.enter_context(tc.tile_pool(name="w", bufs=HEADS))
         stage = stack.enter_context(tc.tile_pool(name="stage", bufs=2))
         stats = stack.enter_context(tc.tile_pool(name="stats", bufs=3))
-        ring = stack.enter_context(tc.tile_pool(name="ring", bufs=3))
-        results = stack.enter_context(tc.tile_pool(name="results", bufs=4))
+        results = stack.enter_context(tc.tile_pool(name="results", bufs=3))
+        work = stack.enter_context(tc.tile_pool(name="work", bufs=2))
         psum_turn = stack.enter_context(tc.psum_pool(name="psum_turn", bufs=2 * TILES_PER_ROUND))
-        psum_prod = stack.enter_context(tc.psum_pool(name="psum_prod", bufs=2 * TILES_PER_ROUND))
+        psum_prod = stack.enter_context(tc.psum_pool(name="psum_prod", bufs=2))
 
         gain_rows = consts.tile([P, 2, D], BF16)
         nc.vector.memset(gain_rows[:], 0.0)
@@ -111,16 +112,18 @@ def tile_refattention_pa_t_kernel(
         def side_by_side(turned):
             return turned[:].rearrange("p (g u) r -> p g r u", u=2)
 
-        w_grouped = consts.tile([P, PASSES, FEATURES, PACK], BF16, align_bytes=64)
-        w_grouped_words = w_grouped[:].bitcast(F32)
         w_words = w_raw[:].bitcast(F32)
         w_codes = consts.tile([P, PASSES, FEATURES], U32, align_bytes=64)
         w_scales = consts.tile([P, PASSES, FEATURES], U8, align_bytes=64)
 
+        w_grouped_of = {}
+
         def prepare_head(h):
             turned = turn(w_words[:, h, :])
+            w_grouped = w_pool.tile([P, PASSES, D, PACK], BF16, align_bytes=64)
+            w_grouped_of[h] = w_grouped
             copy_out = nc.scalar.copy if h % 2 == 0 else nc.vector.tensor_copy
-            copy_out(out=w_grouped_words[:, :, h * D : (h + 1) * D, :], in_=side_by_side(turned))
+            copy_out(out=w_grouped[:].bitcast(F32), in_=side_by_side(turned))
 
         def quantise_head(h):
             columns = slice(h * D, (h + 1) * D)
@@ -128,7 +131,7 @@ def tile_refattention_pa_t_kernel(
                 nc.vector.quantize_mx(
                     out=w_codes[:, g, columns].bitcast(FP8X4),
                     scales=w_scales[:, g, columns],
-                    in_=w_grouped[:, g, columns, :].rearrange("p f t -> p (f t)"),
+                    in_=w_grouped_of[h][:, g, :, :].rearrange("p f t -> p (f t)"),
                 )
 
         prepare_head(0)
@@ -139,27 +142,36 @@ def tile_refattention_pa_t_kernel(
         for h in range(1, HEADS):
             quantise_head(h)
 
-        gains = consts.tile([P, ROTATED, D], BF16)
-        spread = psum_prod.tile([P, FEATURES], F32, tag="product")
+        low = slice(0, HALF)
+        high = slice(HALF, D)
+        gains = consts.tile([P, 3, D], BF16)
+        spread = psum_prod.tile([P, 2 * TILES_PER_ROUND, D], F32, tag="product_q")
         nc.tensor.matmul(
-            out=spread[:, 0 : 2 * D],
+            out=spread[:, 0:2, :].rearrange("p a d -> p (a d)"),
             lhsT=ones[:],
             rhs=gain_rows[:].rearrange("p a d -> p (a d)"),
             start=True,
             stop=True,
         )
-        nc.vector.tensor_copy(
-            out=gains[:, 0:2, :], in_=spread[:, 0:D].unsqueeze(1).to_broadcast([P, 2, D])
-        )
-        nc.vector.tensor_copy(out=gains[:, 2, :], in_=spread[:, D : 2 * D])
+        nc.vector.tensor_copy(out=gains[:, 0, :], in_=spread[:, 0, :])
+        nc.vector.tensor_copy(out=gains[:, 1, low], in_=spread[:, 0, high])
+        nc.vector.tensor_copy(out=gains[:, 1, high], in_=spread[:, 0, low])
+        nc.vector.tensor_copy(out=gains[:, 2, :], in_=spread[:, 1, :])
 
         turned_of = {}
         grouped_of = {}
         codes_of = {}
-        product_of = {}
-        gained_of = {}
-        result_of = {}
-        normed_of = {}
+        q_of = {}
+        kv_of = {}
+        sums_of = {}
+        rstd_of = {}
+        work_of = {}
+        k_gained_of = {}
+        rotated_of = {}
+
+        def tiles_of(r):
+            first = r * TILES_PER_ROUND
+            return slice(first, first + TILES_PER_ROUND)
 
         def transpose_tokens(r):
             x_words = x_of[r][:].bitcast(F32)
@@ -185,122 +197,154 @@ def tile_refattention_pa_t_kernel(
 
         def project(r):
             codes, scales = codes_of[r]
-            product_of[r] = []
+            product_q = psum_prod.tile([P, TILES_PER_ROUND * 2, D], F32)
+            product_kv = psum_prod.tile([P, TILES_PER_ROUND * 2, D], F32)
             for t in range(TILES_PER_ROUND):
-                product = psum_prod.tile([P, FEATURES], F32, tag="product")
-                for g in range(PASSES):
-                    nc.tensor.matmul_mx(
-                        out=product[:],
-                        lhsT=codes[:, t, g, :].bitcast(FP8X4),
-                        lhsT_scale=scales[:, t, g, :],
-                        rhs=w_codes[:, g, :].bitcast(FP8X4),
-                        rhs_scale=w_scales[:, g, :],
-                        start=(g == 0),
-                        stop=(g == PASSES - 1),
+                for product, first in ((product_q, 0), (product_kv, 2 * D)):
+                    for g in range(PASSES):
+                        nc.tensor.matmul_mx(
+                            out=product[:, 2 * t : 2 * t + 2, :].rearrange("p h d -> p (h d)"),
+                            lhsT=codes[:, t, g, :].bitcast(FP8X4),
+                            lhsT_scale=scales[:, t, g, :],
+                            rhs=w_codes[:, g, first : first + 2 * D].bitcast(FP8X4),
+                            rhs_scale=w_scales[:, g, first : first + 2 * D],
+                            start=(g == 0),
+                            stop=(g == PASSES - 1),
+                        )
+            q_of[r] = product_q[:].rearrange("p (t h) d -> p t h d", h=2)
+            kv_of[r] = product_kv[:].rearrange("p (t h) d -> p t h d", h=2)
+
+        def sum_squares(r, first_head):
+            if r not in sums_of:
+                sums = stats.tile([P, TILES_PER_ROUND, HEADS], F32)
+                squares = stats.tile([P, TILES_PER_ROUND, HEADS, D], BF16)
+                sums_of[r] = (sums, squares)
+            sums, squares = sums_of[r]
+            product = q_of[r] if first_head == 0 else kv_of[r]
+            for t in range(TILES_PER_ROUND):
+                for a in range(2):
+                    nc.scalar.activation(
+                        out=squares[:, t, first_head + a, :],
+                        in_=product[:, t, a, :],
+                        func=ACT.Square,
+                        accum_out=sums[:, t, first_head + a : first_head + a + 1],
                     )
-                product_of[r].append(product)
 
-        def normalise(r):
-            sum_sq = stats.tile([P, TILES_PER_ROUND, HEADS], F32)
+        def reciprocal_rms(r):
             rstd = stats.tile([P, TILES_PER_ROUND, HEADS], F32)
-            squares = stage.tile([P, TILES_PER_ROUND, HEADS, D], BF16)
-            normed = ring.tile([P, ROTATED, TILES_PER_ROUND, D], F32)
-            result = results.tile([P, HEADS, TILES_PER_ROUND, D], F32)
+            nc.scalar.activation(
+                out=rstd[:], in_=sums_of[r][0][:], func=ACT.Abs_reciprocal_sqrt, scale=1.0 / D, bias=eps[:]
+            )
+            rstd_of[r] = rstd
 
-            def sum_squares(t, h):
-                nc.scalar.activation(
-                    out=squares[:, t, h, :],
-                    in_=product_of[r][t][:, h * D : (h + 1) * D],
-                    func=ACT.Square,
-                    accum_out=sum_sq[:, t, h : h + 1],
+        def fold_tables(r):
+            parts = work.tile([P, 2 * TILES_PER_ROUND * D + 2 * TILES_PER_ROUND * ROTATED * D], F32)
+            n = TILES_PER_ROUND * D
+            q_cos = parts[:, 0:n].rearrange("p (t d) -> p t d", d=D)
+            q_sin = parts[:, n : 2 * n].rearrange("p (t d) -> p t d", d=D)
+            m = ROTATED * n
+            with_cos = parts[:, 2 * n : 2 * n + m].rearrange("p (t h d) -> p t h d", h=ROTATED, d=D)
+            with_sin = parts[:, 2 * n + m : 2 * n + 2 * m].rearrange("p (t h d) -> p t h d", h=ROTATED, d=D)
+            for out, table, a in ((q_cos, cos_sb, 0), (q_sin, sin_sb, 1)):
+                nc.gpsimd.tensor_tensor(
+                    out=out,
+                    in0=table[:, tiles_of(r), :],
+                    in1=gains[:, a, :].unsqueeze(1).to_broadcast([P, TILES_PER_ROUND, D]),
+                    op=ALU.mult,
                 )
+            work_of[r] = (q_cos, q_sin, with_cos, with_sin)
 
-            def reciprocal_rms(t):
-                nc.scalar.activation(
-                    out=rstd[:, t, :], in_=sum_sq[:, t, :], func=ACT.Abs_reciprocal_sqrt, scale=1.0 / D, bias=eps[:]
+        def times(out, in0, in1):
+            nc.vector.tensor_tensor(out=out, in0=in0, in1=in1, op=ALU.mult)
+
+        def multiply(r):
+            q, kv = q_of[r], kv_of[r]
+            q_cos, q_sin, with_cos, with_sin = work_of[r]
+
+            def both(table):
+                return table.unsqueeze(2).to_broadcast([P, TILES_PER_ROUND, 2, table.shape[-1]])
+
+            k_gained = stats.tile([P, TILES_PER_ROUND, D], F32)
+            times(with_cos[:, :, 0:2, :], q, both(q_cos))
+            times(with_sin[:, :, 0:2, low], q[:, :, :, high], both(q_sin[:, :, low]))
+            times(k_gained[:], kv[:, :, 0, :], gains[:, 2, :].unsqueeze(1).to_broadcast([P, TILES_PER_ROUND, D]))
+            times(with_sin[:, :, 0:2, high], q[:, :, :, low], both(q_sin[:, :, high]))
+            times(with_cos[:, :, 2, :], k_gained[:], cos_sb[:, tiles_of(r), :])
+            times(with_sin[:, :, 2, low], k_gained[:, :, high], sin_sb[:, tiles_of(r), low])
+            times(with_sin[:, :, 2, high], k_gained[:, :, low], sin_sb[:, tiles_of(r), high])
+
+        def join(r):
+            q_cos, q_sin, with_cos, with_sin = work_of[r]
+            rotated = stats.tile([P, TILES_PER_ROUND, ROTATED, D], F32)
+            for half, op in ((low, ALU.subtract), (high, ALU.add)):
+                nc.vector.tensor_tensor(
+                    out=rotated[:, :, :, half], in0=with_cos[:, :, :, half], in1=with_sin[:, :, :, half], op=op
                 )
+            rotated_of[r] = rotated
 
-            def times_rstd(t, h):
+        def finish_q(r, t, q_out):
+            for h in range(2):
                 nc.scalar.activation(
-                    out=result[:, V_HEAD, t, :] if h == V_HEAD else normed[:, h, t, :],
-                    in_=product_of[r][t][:, h * D : (h + 1) * D],
+                    out=q_out[:, h, t, :],
+                    in_=rotated_of[r][:, t, h, :],
                     func=ACT.Copy,
-                    scale=rstd[:, t, h : h + 1],
+                    scale=rstd_of[r][:, t, h : h + 1],
                 )
 
-            every = [(t, h) for t in range(TILES_PER_ROUND) for h in range(HEADS)]
-            for t, h in every[:-2]:
-                sum_squares(t, h)
-            reciprocal_rms(0)
-            for t, h in every[-2:]:
-                sum_squares(t, h)
-            for t, h in every[: HEADS - 1]:
-                times_rstd(t, h)
-            reciprocal_rms(1)
-            for t, h in every[HEADS - 1 :]:
-                times_rstd(t, h)
-            normed_of[r] = normed
-            result_of[r] = result
+        def finish_k(r):
+            k_out = results.tile([P, TILES_PER_ROUND, D], F32)
+            for t in range(TILES_PER_ROUND):
+                nc.vector.tensor_scalar(
+                    out=k_out[:, t, :],
+                    in0=rotated_of[r][:, t, 2, :],
+                    scalar1=rstd_of[r][:, t, 2:3],
+                    scalar2=None,
+                    op0=ALU.mult,
+                )
+            nc.sync.dma_start(out=k_view[:, tiles_of(r), :], in_=k_out[:])
 
-        def apply_gains(r):
-            gained = stage.tile([P, ROTATED, TILES_PER_ROUND, D], F32)
-            nc.vector.tensor_tensor(
-                out=gained[:],
-                in0=normed_of[r][:],
-                in1=gains[:].unsqueeze(2).to_broadcast([P, ROTATED, TILES_PER_ROUND, D]),
-                op=ALU.mult,
-            )
-            gained_of[r] = gained
-
-        def rotate_and_store(r):
-            first = r * TILES_PER_ROUND
-            tiles = slice(first, first + TILES_PER_ROUND)
-            low = slice(0, HALF)
-            high = slice(HALF, D)
-            result = result_of[r]
-
-            def over_heads(table, columns, width):
-                return table[:, tiles, columns].unsqueeze(1).to_broadcast([P, ROTATED, TILES_PER_ROUND, width])
-
-            gained = gained_of[r]
-            with_cos = stage.tile([P, ROTATED, TILES_PER_ROUND, D], F32)
-            with_sin = stage.tile([P, ROTATED, TILES_PER_ROUND, D], F32)
-            nc.vector.tensor_tensor(out=with_cos[:], in0=gained[:], in1=over_heads(cos_sb, slice(0, D), D), op=ALU.mult)
-            nc.vector.tensor_tensor(
-                out=with_sin[:, :, :, low], in0=gained[:, :, :, high], in1=over_heads(sin_sb, low, HALF), op=ALU.mult
-            )
-            nc.vector.tensor_tensor(
-                out=with_sin[:, :, :, high], in0=gained[:, :, :, low], in1=over_heads(sin_sb, high, HALF), op=ALU.mult
-            )
-            nc.vector.tensor_tensor(
-                out=result[:, 0:ROTATED, :, low], in0=with_cos[:, :, :, low], in1=with_sin[:, :, :, low], op=ALU.subtract
-            )
-            nc.vector.tensor_tensor(
-                out=result[:, 0:ROTATED, :, high], in0=with_cos[:, :, :, high], in1=with_sin[:, :, :, high], op=ALU.add
-            )
-            nc.sync.dma_start(out=q_view[:, :, tiles, :], in_=result[:, 0:2, :, :])
-            nc.sync.dma_start(out=k_view[:, tiles, :], in_=result[:, 2, :, :])
-            nc.sync.dma_start(out=v_view[:, tiles, :], in_=result[:, V_HEAD, :, :])
+        def finish_v(r):
+            v_out = results.tile([P, TILES_PER_ROUND, D], F32)
+            for t in range(TILES_PER_ROUND):
+                nc.scalar.activation(
+                    out=v_out[:, t, :],
+                    in_=kv_of[r][:, t, 1, :],
+                    func=ACT.Copy,
+                    scale=rstd_of[r][:, t, V_HEAD : V_HEAD + 1],
+                )
+            nc.sync.dma_start(out=v_view[:, tiles_of(r), :], in_=v_out[:])
 
         def in_range(r):
             return 0 <= r < ROUNDS
 
-        for i in range(-3, ROUNDS):
+        for i in range(-3, ROUNDS + 1):
             if in_range(i + LOAD_AHEAD):
                 load_tokens(i + LOAD_AHEAD)
             if i == -2:
                 load_tables(TABLE_SPLIT, TILES)
             if in_range(i + 1):
                 project(i + 1)
+                fold_tables(i + 1)
             if in_range(i + 3):
                 transpose_tokens(i + 3)
+            if in_range(i):
+                sum_squares(i, 2)
+                multiply(i)
             if in_range(i + 2):
                 regroup(i + 2)
-            if in_range(i + 1):
-                normalise(i + 1)
             if in_range(i):
-                apply_gains(i)
+                sum_squares(i, 0)
+            if in_range(i - 1):
+                q_out = results.tile([P, 2, TILES_PER_ROUND, D], F32)
+                finish_q(i - 1, 0, q_out)
+            if in_range(i):
+                reciprocal_rms(i)
+            if in_range(i - 1):
+                finish_q(i - 1, 1, q_out)
+                nc.sync.dma_start(out=q_view[:, :, tiles_of(i - 1), :], in_=q_out[:])
+                finish_k(i - 1)
             if in_range(i + 2):
                 quantise(i + 2)
             if in_range(i):
-                rotate_and_store(i)
+                finish_v(i)
+                join(i)

@@ -80,12 +80,11 @@ def tile_refattention_pa_t_kernel(
                 nc.sync.dma_start(out=x_sb[:, t : t + step, :], in_=x_view[:, first + t : first + t + step, :])
             x_of[r] = x_sb
 
-        cos_sb = consts.tile([P, TILES, D], BF16)
-        sin_sb = consts.tile([P, TILES, D], BF16)
+        tables = consts.tile([P, 2, TILES, D], BF16)
 
         def load_tables(first, last):
-            nc.sync.dma_start(out=cos_sb[:, first:last, :], in_=cos_view[:, first:last, :])
-            nc.sync.dma_start(out=sin_sb[:, first:last, :], in_=sin_view[:, first:last, :])
+            for a, view in enumerate((cos_view, sin_view)):
+                nc.sync.dma_start(out=tables[:, a, first:last, :], in_=view[:, first:last, :])
 
         load_tokens(0)
         load_tokens(1)
@@ -238,47 +237,48 @@ def tile_refattention_pa_t_kernel(
             rstd_of[r] = rstd
 
         def fold_tables(r):
-            parts = work.tile([P, 2 * TILES_PER_ROUND * D + 2 * TILES_PER_ROUND * ROTATED * D], F32)
-            n = TILES_PER_ROUND * D
-            q_cos = parts[:, 0:n].rearrange("p (t d) -> p t d", d=D)
-            q_sin = parts[:, n : 2 * n].rearrange("p (t d) -> p t d", d=D)
-            m = ROTATED * n
-            with_cos = parts[:, 2 * n : 2 * n + m].rearrange("p (t h d) -> p t h d", h=ROTATED, d=D)
-            with_sin = parts[:, 2 * n + m : 2 * n + 2 * m].rearrange("p (t h d) -> p t h d", h=ROTATED, d=D)
-            for out, table, a in ((q_cos, cos_sb, 0), (q_sin, sin_sb, 1)):
-                nc.gpsimd.tensor_tensor(
-                    out=out,
-                    in0=table[:, tiles_of(r), :],
-                    in1=gains[:, a, :].unsqueeze(1).to_broadcast([P, TILES_PER_ROUND, D]),
-                    op=ALU.mult,
-                )
-            work_of[r] = (q_cos, q_sin, with_cos, with_sin)
+            parts = work.tile([P, 2 * TILES_PER_ROUND + TILES_PER_ROUND * ROTATED // 2, D], F32)
+            folded = parts[:, 0 : 2 * TILES_PER_ROUND, :].rearrange("p (a t) d -> p a t d", a=2)
+            nc.gpsimd.tensor_tensor(
+                out=folded,
+                in0=tables[:, :, tiles_of(r), :],
+                in1=gains[:, 0:2, :].unsqueeze(2).to_broadcast([P, 2, TILES_PER_ROUND, D]),
+                op=ALU.mult,
+            )
+            sin_low = (
+                parts[:, 2 * TILES_PER_ROUND :, :]
+                .rearrange("p n d -> p (n d)")
+                .rearrange("p (t h d) -> p t h d", h=ROTATED, d=HALF)
+            )
+            sin_high = work.tile([P, TILES_PER_ROUND, ROTATED, HALF], F32)
+            with_cos = work.tile([P, TILES_PER_ROUND, ROTATED, D], F32)
+            work_of[r] = (folded, with_cos, sin_low, sin_high)
 
         def times(out, in0, in1):
             nc.vector.tensor_tensor(out=out, in0=in0, in1=in1, op=ALU.mult)
 
         def multiply(r):
             q, kv = q_of[r], kv_of[r]
-            q_cos, q_sin, with_cos, with_sin = work_of[r]
+            folded, with_cos, sin_low, sin_high = work_of[r]
 
             def both(table):
                 return table.unsqueeze(2).to_broadcast([P, TILES_PER_ROUND, 2, table.shape[-1]])
 
             k_gained = stats.tile([P, TILES_PER_ROUND, D], F32)
-            times(with_cos[:, :, 0:2, :], q, both(q_cos))
-            times(with_sin[:, :, 0:2, low], q[:, :, :, high], both(q_sin[:, :, low]))
+            times(with_cos[:, :, 0:2, :], q, both(folded[:, 0, :, :]))
+            times(sin_low[:, :, 0:2, :], q[:, :, :, high], both(folded[:, 1, :, low]))
             times(k_gained[:], kv[:, :, 0, :], gains[:, 2, :].unsqueeze(1).to_broadcast([P, TILES_PER_ROUND, D]))
-            times(with_sin[:, :, 0:2, high], q[:, :, :, low], both(q_sin[:, :, high]))
-            times(with_cos[:, :, 2, :], k_gained[:], cos_sb[:, tiles_of(r), :])
-            times(with_sin[:, :, 2, low], k_gained[:, :, high], sin_sb[:, tiles_of(r), low])
-            times(with_sin[:, :, 2, high], k_gained[:, :, low], sin_sb[:, tiles_of(r), high])
+            times(sin_high[:, :, 0:2, :], q[:, :, :, low], both(folded[:, 1, :, high]))
+            times(with_cos[:, :, 2, :], k_gained[:], tables[:, 0, tiles_of(r), :])
+            times(sin_low[:, :, 2, :], k_gained[:, :, high], tables[:, 1, tiles_of(r), low])
+            times(sin_high[:, :, 2, :], k_gained[:, :, low], tables[:, 1, tiles_of(r), high])
 
         def join(r):
-            q_cos, q_sin, with_cos, with_sin = work_of[r]
+            folded, with_cos, sin_low, sin_high = work_of[r]
             rotated = stats.tile([P, TILES_PER_ROUND, ROTATED, D], F32)
-            for half, op in ((low, ALU.subtract), (high, ALU.add)):
+            for half, with_sin, op in ((low, sin_low, ALU.subtract), (high, sin_high[:], ALU.add)):
                 nc.vector.tensor_tensor(
-                    out=rotated[:, :, :, half], in0=with_cos[:, :, :, half], in1=with_sin[:, :, :, half], op=op
+                    out=rotated[:, :, :, half], in0=with_cos[:, :, :, half], in1=with_sin, op=op
                 )
             rotated_of[r] = rotated
 

@@ -32,7 +32,7 @@ TILES = TOKENS // P
 TILES_PER_ROUND = 2
 ROUNDS = TILES // TILES_PER_ROUND
 LOAD_AHEAD = 6
-TABLE_SPLIT = 4 * TILES_PER_ROUND
+TABLE_SPLITS = (4, 12)
 
 FLOPS = 2 * TOKENS * HID * FEATURES
 
@@ -61,14 +61,17 @@ def tile_refattention_pa_t_kernel(
         psum_turn = stack.enter_context(tc.psum_pool(name="psum_turn", bufs=2 * TILES_PER_ROUND))
         psum_prod = stack.enter_context(tc.psum_pool(name="psum_prod", bufs=2))
 
+        identity = consts.tile([P, P], F32)
+        make_identity(nc, identity[:])
+
         gain_rows = consts.tile([P, 2, D], BF16)
         nc.vector.memset(gain_rows[:], 0.0)
-        for a, w in enumerate((q_norm_w, k_norm_w)):
-            nc.scalar.dma_start(out=gain_rows[0:1, a, :], in_=w.rearrange("(o d) -> o d", o=1))
 
         w_raw = consts.tile([P, HEADS, HID], BF16)
-        for h, rows in enumerate((Wq[0:D, :], Wq[D : 2 * D, :], Wk, Wv)):
-            nc.sync.dma_start(out=w_raw[:, h, :], in_=rows)
+        w_rows = (Wq[0:D, :], Wq[D : 2 * D, :], Wk, Wv)
+
+        def load_head(h):
+            nc.sync.dma_start(out=w_raw[:, h, :], in_=w_rows[h])
 
         x_of = {}
 
@@ -86,13 +89,23 @@ def tile_refattention_pa_t_kernel(
             for a, view in enumerate((cos_view, sin_view)):
                 nc.sync.dma_start(out=tables[:, a, first:last, :], in_=view[:, first:last, :])
 
+        load_head(0)
+        load_head(1)
+        for a, w in enumerate((q_norm_w, k_norm_w)):
+            nc.sync.dma_start(out=gain_rows[0:1, a, :], in_=w.rearrange("(o d) -> o d", o=1))
         load_tokens(0)
+        load_head(2)
+        load_head(3)
+        load_tables(0, TABLE_SPLITS[0])
         load_tokens(1)
-        load_tables(0, TABLE_SPLIT)
+        load_tables(TABLE_SPLITS[0], TABLE_SPLITS[1])
         load_tokens(2)
+        load_tokens(3)
+        load_tables(TABLE_SPLITS[1], TILES)
+        load_tokens(4)
+        load_tokens(5)
+        load_tokens(6)
 
-        identity = consts.tile([P, P], F32)
-        make_identity(nc, identity[:])
         eps = consts.tile([P, 1], F32)
         nc.vector.memset(eps[:], EPS)
         ones = consts.tile([P, P], BF16)
@@ -117,11 +130,10 @@ def tile_refattention_pa_t_kernel(
 
         w_grouped_of = {}
 
-        def prepare_head(h):
+        def prepare_head(h, copy_out):
             turned = turn(w_words[:, h, :])
             w_grouped = w_pool.tile([P, PASSES, D, PACK], BF16, align_bytes=64)
             w_grouped_of[h] = w_grouped
-            copy_out = nc.scalar.copy if h % 2 == 0 else nc.vector.tensor_copy
             copy_out(out=w_grouped[:].bitcast(F32), in_=side_by_side(turned))
 
         def quantise_head(h):
@@ -133,29 +145,24 @@ def tile_refattention_pa_t_kernel(
                     in_=w_grouped_of[h][:, g, :, :].rearrange("p f t -> p (f t)"),
                 )
 
-        prepare_head(0)
-        prepare_head(1)
-        quantise_head(0)
-        prepare_head(2)
-        prepare_head(3)
-        for h in range(1, HEADS):
-            quantise_head(h)
 
         low = slice(0, HALF)
         high = slice(HALF, D)
         gains = consts.tile([P, 3, D], BF16)
-        spread = psum_prod.tile([P, 2 * TILES_PER_ROUND, D], F32, tag="product_q")
-        nc.tensor.matmul(
-            out=spread[:, 0:2, :].rearrange("p a d -> p (a d)"),
-            lhsT=ones[:],
-            rhs=gain_rows[:].rearrange("p a d -> p (a d)"),
-            start=True,
-            stop=True,
-        )
-        nc.vector.tensor_copy(out=gains[:, 0, :], in_=spread[:, 0, :])
-        nc.vector.tensor_copy(out=gains[:, 1, low], in_=spread[:, 0, high])
-        nc.vector.tensor_copy(out=gains[:, 1, high], in_=spread[:, 0, low])
-        nc.vector.tensor_copy(out=gains[:, 2, :], in_=spread[:, 1, :])
+
+        def spread_gains():
+            spread = psum_prod.tile([P, 2 * TILES_PER_ROUND, D], F32, tag="product_kv")
+            nc.tensor.matmul(
+                out=spread[:, 0:2, :].rearrange("p a d -> p (a d)"),
+                lhsT=ones[:],
+                rhs=gain_rows[:].rearrange("p a d -> p (a d)"),
+                start=True,
+                stop=True,
+            )
+            nc.vector.tensor_copy(out=gains[:, 0, :], in_=spread[:, 0, :])
+            nc.vector.tensor_copy(out=gains[:, 1, low], in_=spread[:, 0, high])
+            nc.vector.tensor_copy(out=gains[:, 1, high], in_=spread[:, 0, low])
+            nc.vector.tensor_copy(out=gains[:, 2, :], in_=spread[:, 1, :])
 
         turned_of = {}
         grouped_of = {}
@@ -180,38 +187,45 @@ def tile_refattention_pa_t_kernel(
             grouped = stage.tile([P, TILES_PER_ROUND, PASSES, P, PACK], BF16, align_bytes=64)
             grouped_words = grouped[:].bitcast(F32)
             for t in range(TILES_PER_ROUND):
-                copy_out = nc.vector.tensor_copy if r == 0 and t == 0 else nc.scalar.copy
+                copy_out = nc.vector.tensor_copy if (r, t) == (0, 1) else nc.scalar.copy
                 copy_out(out=grouped_words[:, t], in_=side_by_side(turned_of[r][t]))
             grouped_of[r] = grouped
 
         def quantise(r):
             codes = stats.tile([P, TILES_PER_ROUND, PASSES, P], U32, align_bytes=64)
             scales = stats.tile([P, TILES_PER_ROUND, PASSES, P], U8, align_bytes=64)
-            nc.vector.quantize_mx(
-                out=codes[:].rearrange("p t g r -> p (t g r)").bitcast(FP8X4),
-                scales=scales[:].rearrange("p t g r -> p (t g r)"),
-                in_=grouped_of[r][:].rearrange("p t g r v -> p (t g r v)"),
-            )
+            step = 1 if r == 0 else TILES_PER_ROUND
+            for t in range(0, TILES_PER_ROUND, step):
+                span = slice(t, t + step)
+                nc.vector.quantize_mx(
+                    out=codes[:, span].rearrange("p t g r -> p (t g r)").bitcast(FP8X4),
+                    scales=scales[:, span].rearrange("p t g r -> p (t g r)"),
+                    in_=grouped_of[r][:, span].rearrange("p t g r v -> p (t g r v)"),
+                )
             codes_of[r] = (codes, scales)
 
-        def project(r):
+        def project(r, of, first):
             codes, scales = codes_of[r]
-            product_q = psum_prod.tile([P, TILES_PER_ROUND * 2, D], F32)
-            product_kv = psum_prod.tile([P, TILES_PER_ROUND * 2, D], F32)
+            product = psum_prod.tile([P, TILES_PER_ROUND * 2, D], F32, tag="product_q" if first == 0 else "product_kv")
+            columns = slice(first * D, (first + 2) * D)
             for t in range(TILES_PER_ROUND):
-                for product, first in ((product_q, 0), (product_kv, 2 * D)):
-                    for g in range(PASSES):
-                        nc.tensor.matmul_mx(
-                            out=product[:, 2 * t : 2 * t + 2, :].rearrange("p h d -> p (h d)"),
-                            lhsT=codes[:, t, g, :].bitcast(FP8X4),
-                            lhsT_scale=scales[:, t, g, :],
-                            rhs=w_codes[:, g, first : first + 2 * D].bitcast(FP8X4),
-                            rhs_scale=w_scales[:, g, first : first + 2 * D],
-                            start=(g == 0),
-                            stop=(g == PASSES - 1),
-                        )
-            q_of[r] = product_q[:].rearrange("p (t h) d -> p t h d", h=2)
-            kv_of[r] = product_kv[:].rearrange("p (t h) d -> p t h d", h=2)
+                for g in range(PASSES):
+                    nc.tensor.matmul_mx(
+                        out=product[:, 2 * t : 2 * t + 2, :].rearrange("p h d -> p (h d)"),
+                        lhsT=codes[:, t, g, :].bitcast(FP8X4),
+                        lhsT_scale=scales[:, t, g, :],
+                        rhs=w_codes[:, g, columns].bitcast(FP8X4),
+                        rhs_scale=w_scales[:, g, columns],
+                        start=(g == 0),
+                        stop=(g == PASSES - 1),
+                    )
+            of[r] = product[:].rearrange("p (t h) d -> p t h d", h=2)
+
+        def project_q(r):
+            project(r, q_of, 0)
+
+        def project_kv(r):
+            project(r, kv_of, 2)
 
         def sum_squares(r, first_head):
             if r not in sums_of:
@@ -239,7 +253,8 @@ def tile_refattention_pa_t_kernel(
         def fold_tables(r):
             parts = work.tile([P, 2 * TILES_PER_ROUND + TILES_PER_ROUND * ROTATED // 2, D], F32)
             folded = parts[:, 0 : 2 * TILES_PER_ROUND, :].rearrange("p (a t) d -> p a t d", a=2)
-            nc.gpsimd.tensor_tensor(
+            engine = nc.vector if r == 0 else nc.gpsimd
+            engine.tensor_tensor(
                 out=folded,
                 in0=tables[:, :, tiles_of(r), :],
                 in1=gains[:, 0:2, :].unsqueeze(2).to_broadcast([P, 2, TILES_PER_ROUND, D]),
@@ -257,18 +272,28 @@ def tile_refattention_pa_t_kernel(
         def times(out, in0, in1):
             nc.vector.tensor_tensor(out=out, in0=in0, in1=in1, op=ALU.mult)
 
-        def multiply(r):
-            q, kv = q_of[r], kv_of[r]
+        def both(table):
+            return table.unsqueeze(2).to_broadcast([P, TILES_PER_ROUND, 2, table.shape[-1]])
+
+        def multiply_q_cos(r):
             folded, with_cos, sin_low, sin_high = work_of[r]
+            times(with_cos[:, :, 0:2, :], q_of[r], both(folded[:, 0, :, :]))
 
-            def both(table):
-                return table.unsqueeze(2).to_broadcast([P, TILES_PER_ROUND, 2, table.shape[-1]])
+        def multiply_q_sin(r, half):
+            folded, with_cos, sin_low, sin_high = work_of[r]
+            if half == low:
+                times(sin_low[:, :, 0:2, :], q_of[r][:, :, :, high], both(folded[:, 1, :, low]))
+            else:
+                times(sin_high[:, :, 0:2, :], q_of[r][:, :, :, low], both(folded[:, 1, :, high]))
 
+        def gain_k(r):
             k_gained = stats.tile([P, TILES_PER_ROUND, D], F32)
-            times(with_cos[:, :, 0:2, :], q, both(folded[:, 0, :, :]))
-            times(sin_low[:, :, 0:2, :], q[:, :, :, high], both(folded[:, 1, :, low]))
-            times(k_gained[:], kv[:, :, 0, :], gains[:, 2, :].unsqueeze(1).to_broadcast([P, TILES_PER_ROUND, D]))
-            times(sin_high[:, :, 0:2, :], q[:, :, :, low], both(folded[:, 1, :, high]))
+            times(k_gained[:], kv_of[r][:, :, 0, :], gains[:, 2, :].unsqueeze(1).to_broadcast([P, TILES_PER_ROUND, D]))
+            k_gained_of[r] = k_gained
+
+        def multiply_k(r):
+            folded, with_cos, sin_low, sin_high = work_of[r]
+            k_gained = k_gained_of[r]
             times(with_cos[:, :, 2, :], k_gained[:], tables[:, 0, tiles_of(r), :])
             times(sin_low[:, :, 2, :], k_gained[:, :, high], tables[:, 1, tiles_of(r), low])
             times(sin_high[:, :, 2, :], k_gained[:, :, low], tables[:, 1, tiles_of(r), high])
@@ -276,32 +301,58 @@ def tile_refattention_pa_t_kernel(
         def join(r):
             folded, with_cos, sin_low, sin_high = work_of[r]
             rotated = stats.tile([P, TILES_PER_ROUND, ROTATED, D], F32)
-            for half, with_sin, op in ((low, sin_low, ALU.subtract), (high, sin_high[:], ALU.add)):
-                nc.vector.tensor_tensor(
-                    out=rotated[:, :, :, half], in0=with_cos[:, :, :, half], in1=with_sin, op=op
-                )
+            step = 1 if r == ROUNDS - 1 else TILES_PER_ROUND
+            for t in range(0, TILES_PER_ROUND, step):
+                span = slice(t, t + step)
+                for half, with_sin, op in ((low, sin_low, ALU.subtract), (high, sin_high[:], ALU.add)):
+                    nc.vector.tensor_tensor(
+                        out=rotated[:, span, :, half],
+                        in0=with_cos[:, span, :, half],
+                        in1=with_sin[:, span, :, :],
+                        op=op,
+                    )
             rotated_of[r] = rotated
+
+        def times_rstd_on_scalar(out, r, t, h):
+            nc.scalar.activation(
+                out=out, in_=rotated_of[r][:, t, h, :], func=ACT.Copy, scale=rstd_of[r][:, t, h : h + 1]
+            )
+
+        def times_rstd_on_vector(out, r, t, h):
+            nc.vector.tensor_scalar(
+                out=out,
+                in0=rotated_of[r][:, t, h, :],
+                scalar1=rstd_of[r][:, t, h : h + 1],
+                scalar2=None,
+                op0=ALU.mult,
+            )
 
         def finish_q(r, t, q_out):
             for h in range(2):
-                nc.scalar.activation(
-                    out=q_out[:, h, t, :],
-                    in_=rotated_of[r][:, t, h, :],
-                    func=ACT.Copy,
-                    scale=rstd_of[r][:, t, h : h + 1],
-                )
+                times_rstd_on_scalar(q_out[:, h, t, :], r, t, h)
 
         def finish_k(r):
             k_out = results.tile([P, TILES_PER_ROUND, D], F32)
             for t in range(TILES_PER_ROUND):
-                nc.vector.tensor_scalar(
-                    out=k_out[:, t, :],
-                    in0=rotated_of[r][:, t, 2, :],
-                    scalar1=rstd_of[r][:, t, 2:3],
-                    scalar2=None,
-                    op0=ALU.mult,
-                )
+                times_rstd_on_vector(k_out[:, t, :], r, t, 2)
             nc.sync.dma_start(out=k_view[:, tiles_of(r), :], in_=k_out[:])
+
+        def finish_last(r):
+            q_first = results.tile([P, 2, D], F32)
+            q_head_0 = results.tile([P, D], F32)
+            q_head_1 = results.tile([P, D], F32)
+            k_out = results.tile([P, TILES_PER_ROUND, D], F32)
+            t0, t1 = r * TILES_PER_ROUND, r * TILES_PER_ROUND + 1
+            for h in range(2):
+                times_rstd_on_scalar(q_first[:, h, :], r, 0, h)
+            nc.sync.dma_start(out=q_view[:, :, t0, :], in_=q_first[:])
+            times_rstd_on_scalar(q_head_0[:], r, 1, 0)
+            nc.sync.dma_start(out=q_view[:, 0, t1, :], in_=q_head_0[:])
+            for t in range(TILES_PER_ROUND):
+                times_rstd_on_vector(k_out[:, t, :], r, t, 2)
+            nc.sync.dma_start(out=k_view[:, tiles_of(r), :], in_=k_out[:])
+            times_rstd_on_vector(q_head_1[:], r, 1, 1)
+            nc.sync.dma_start(out=q_view[:, 1, t1, :], in_=q_head_1[:])
 
         def finish_v(r):
             v_out = results.tile([P, TILES_PER_ROUND, D], F32)
@@ -317,34 +368,68 @@ def tile_refattention_pa_t_kernel(
         def in_range(r):
             return 0 <= r < ROUNDS
 
-        for i in range(-3, ROUNDS + 1):
+        prepare_head(0, nc.scalar.copy)
+        prepare_head(1, nc.vector.tensor_copy)
+        quantise_head(0)
+        transpose_tokens(0)
+        regroup(0)
+        quantise_head(1)
+        prepare_head(2, nc.scalar.copy)
+        prepare_head(3, nc.scalar.copy)
+        spread_gains()
+        quantise(0)
+        project_q(0)
+        fold_tables(0)
+        quantise_head(2)
+        multiply_q_cos(0)
+        quantise_head(3)
+        transpose_tokens(1)
+        project_kv(0)
+        regroup(1)
+        multiply_q_sin(0, low)
+        multiply_q_sin(0, high)
+        gain_k(0)
+        quantise(1)
+        sum_squares(0, 2)
+        sum_squares(0, 0)
+        transpose_tokens(2)
+        project_q(1)
+        project_kv(1)
+        fold_tables(1)
+        multiply_k(0)
+        regroup(2)
+        transpose_tokens(3)
+        reciprocal_rms(0)
+        finish_v(0)
+        join(0)
+        quantise(2)
+
+        for i in range(1, ROUNDS):
             if in_range(i + LOAD_AHEAD):
                 load_tokens(i + LOAD_AHEAD)
-            if i == -2:
-                load_tables(TABLE_SPLIT, TILES)
             if in_range(i + 1):
-                project(i + 1)
+                project_q(i + 1)
+                project_kv(i + 1)
                 fold_tables(i + 1)
             if in_range(i + 3):
                 transpose_tokens(i + 3)
-            if in_range(i):
-                sum_squares(i, 2)
-                multiply(i)
+            sum_squares(i, 2)
+            multiply_q_cos(i)
+            multiply_q_sin(i, low)
+            gain_k(i)
+            multiply_q_sin(i, high)
+            multiply_k(i)
             if in_range(i + 2):
                 regroup(i + 2)
-            if in_range(i):
-                sum_squares(i, 0)
-            if in_range(i - 1):
-                q_out = results.tile([P, 2, TILES_PER_ROUND, D], F32)
-                finish_q(i - 1, 0, q_out)
-            if in_range(i):
-                reciprocal_rms(i)
-            if in_range(i - 1):
-                finish_q(i - 1, 1, q_out)
-                nc.sync.dma_start(out=q_view[:, :, tiles_of(i - 1), :], in_=q_out[:])
-                finish_k(i - 1)
+            sum_squares(i, 0)
+            q_out = results.tile([P, 2, TILES_PER_ROUND, D], F32)
+            finish_q(i - 1, 0, q_out)
+            reciprocal_rms(i)
+            finish_q(i - 1, 1, q_out)
+            nc.sync.dma_start(out=q_view[:, :, tiles_of(i - 1), :], in_=q_out[:])
+            finish_k(i - 1)
             if in_range(i + 2):
                 quantise(i + 2)
-            if in_range(i):
-                finish_v(i)
-                join(i)
+            finish_v(i)
+            join(i)
+        finish_last(ROUNDS - 1)

@@ -98,8 +98,8 @@ def tile_refattention_pa_t_kernel(
         load_head(3)
         load_tables(0, TABLE_SPLITS[0])
         load_tokens(1)
-        load_tables(TABLE_SPLITS[0], TABLE_SPLITS[1])
         load_tokens(2)
+        load_tables(TABLE_SPLITS[0], TABLE_SPLITS[1])
         load_tokens(3)
         load_tables(TABLE_SPLITS[1], TILES)
         load_tokens(4)
@@ -130,11 +130,11 @@ def tile_refattention_pa_t_kernel(
 
         w_grouped_of = {}
 
-        def prepare_head(h, copy_out):
+        def prepare_head(h):
             turned = turn(w_words[:, h, :])
             w_grouped = w_pool.tile([P, PASSES, D, PACK], BF16, align_bytes=64)
             w_grouped_of[h] = w_grouped
-            copy_out(out=w_grouped[:].bitcast(F32), in_=side_by_side(turned))
+            nc.scalar.copy(out=w_grouped[:].bitcast(F32), in_=side_by_side(turned))
 
         def quantise_head(h):
             columns = slice(h * D, (h + 1) * D)
@@ -152,17 +152,14 @@ def tile_refattention_pa_t_kernel(
 
         def spread_gains():
             spread = psum_prod.tile([P, 2 * TILES_PER_ROUND, D], F32, tag="product_kv")
-            nc.tensor.matmul(
-                out=spread[:, 0:2, :].rearrange("p a d -> p (a d)"),
-                lhsT=ones[:],
-                rhs=gain_rows[:].rearrange("p a d -> p (a d)"),
-                start=True,
-                stop=True,
-            )
-            nc.vector.tensor_copy(out=gains[:, 0, :], in_=spread[:, 0, :])
-            nc.vector.tensor_copy(out=gains[:, 1, low], in_=spread[:, 0, high])
-            nc.vector.tensor_copy(out=gains[:, 1, high], in_=spread[:, 0, low])
-            nc.vector.tensor_copy(out=gains[:, 2, :], in_=spread[:, 1, :])
+            for out, row in (
+                (spread[:, 0, :], gain_rows[:, 0, :]),
+                (spread[:, 1, low], gain_rows[:, 0, high]),
+                (spread[:, 1, high], gain_rows[:, 0, low]),
+                (spread[:, 2, :], gain_rows[:, 1, :]),
+            ):
+                nc.tensor.matmul(out=out, lhsT=ones[:], rhs=row, start=True, stop=True)
+            nc.vector.tensor_copy(out=gains[:], in_=spread[:, 0:3, :])
 
         turned_of = {}
         grouped_of = {}
@@ -187,22 +184,24 @@ def tile_refattention_pa_t_kernel(
             grouped = stage.tile([P, TILES_PER_ROUND, PASSES, P, PACK], BF16, align_bytes=64)
             grouped_words = grouped[:].bitcast(F32)
             for t in range(TILES_PER_ROUND):
-                copy_out = nc.vector.tensor_copy if (r, t) == (0, 1) else nc.scalar.copy
-                copy_out(out=grouped_words[:, t], in_=side_by_side(turned_of[r][t]))
+                nc.scalar.copy(out=grouped_words[:, t], in_=side_by_side(turned_of[r][t]))
             grouped_of[r] = grouped
 
-        def quantise(r):
-            codes = stats.tile([P, TILES_PER_ROUND, PASSES, P], U32, align_bytes=64)
-            scales = stats.tile([P, TILES_PER_ROUND, PASSES, P], U8, align_bytes=64)
-            step = 1 if r == 0 else TILES_PER_ROUND
-            for t in range(0, TILES_PER_ROUND, step):
-                span = slice(t, t + step)
+        def quantise(r, spans):
+            for span in spans:
+                if r not in codes_of:
+                    codes = stats.tile([P, TILES_PER_ROUND, PASSES, P], U32, align_bytes=64)
+                    scales = stats.tile([P, TILES_PER_ROUND, PASSES, P], U8, align_bytes=64)
+                    codes_of[r] = (codes, scales)
+                codes, scales = codes_of[r]
                 nc.vector.quantize_mx(
                     out=codes[:, span].rearrange("p t g r -> p (t g r)").bitcast(FP8X4),
                     scales=scales[:, span].rearrange("p t g r -> p (t g r)"),
                     in_=grouped_of[r][:, span].rearrange("p t g r v -> p (t g r v)"),
                 )
-            codes_of[r] = (codes, scales)
+
+        one_by_one = [slice(t, t + 1) for t in range(TILES_PER_ROUND)]
+        together = [slice(0, TILES_PER_ROUND)]
 
         def project(r, of, first):
             codes, scales = codes_of[r]
@@ -368,31 +367,31 @@ def tile_refattention_pa_t_kernel(
         def in_range(r):
             return 0 <= r < ROUNDS
 
-        prepare_head(0, nc.scalar.copy)
-        prepare_head(1, nc.vector.tensor_copy)
+        prepare_head(0)
         quantise_head(0)
-        transpose_tokens(0)
-        regroup(0)
+        prepare_head(1)
         quantise_head(1)
-        prepare_head(2, nc.scalar.copy)
-        prepare_head(3, nc.scalar.copy)
+        transpose_tokens(0)
         spread_gains()
-        quantise(0)
+        regroup(0)
+        quantise(0, one_by_one)
+        prepare_head(2)
+        prepare_head(3)
         project_q(0)
         fold_tables(0)
         quantise_head(2)
         multiply_q_cos(0)
         quantise_head(3)
         transpose_tokens(1)
-        project_kv(0)
         regroup(1)
         multiply_q_sin(0, low)
         multiply_q_sin(0, high)
-        gain_k(0)
-        quantise(1)
-        sum_squares(0, 2)
         sum_squares(0, 0)
+        project_kv(0)
+        gain_k(0)
+        sum_squares(0, 2)
         transpose_tokens(2)
+        quantise(1, together)
         project_q(1)
         project_kv(1)
         fold_tables(1)
@@ -402,7 +401,7 @@ def tile_refattention_pa_t_kernel(
         reciprocal_rms(0)
         finish_v(0)
         join(0)
-        quantise(2)
+        quantise(2, together)
 
         for i in range(1, ROUNDS):
             if in_range(i + LOAD_AHEAD):
@@ -421,15 +420,21 @@ def tile_refattention_pa_t_kernel(
             multiply_k(i)
             if in_range(i + 2):
                 regroup(i + 2)
-            sum_squares(i, 0)
             q_out = results.tile([P, 2, TILES_PER_ROUND, D], F32)
-            finish_q(i - 1, 0, q_out)
-            reciprocal_rms(i)
-            finish_q(i - 1, 1, q_out)
+            if not in_range(i + 2):
+                finish_q(i - 1, 0, q_out)
+                finish_q(i - 1, 1, q_out)
+                sum_squares(i, 0)
+                reciprocal_rms(i)
+            else:
+                sum_squares(i, 0)
+                finish_q(i - 1, 0, q_out)
+                reciprocal_rms(i)
+                finish_q(i - 1, 1, q_out)
             nc.sync.dma_start(out=q_view[:, :, tiles_of(i - 1), :], in_=q_out[:])
             finish_k(i - 1)
             if in_range(i + 2):
-                quantise(i + 2)
+                quantise(i + 2, together)
             finish_v(i)
             join(i)
         finish_last(ROUNDS - 1)

@@ -78,7 +78,7 @@ def tile_refattention_pa_t_kernel(
         def load_tokens(r):
             x_sb = x_pool.tile([P, TILES_PER_ROUND, HID], BF16)
             first = r * TILES_PER_ROUND
-            step = 1 if r == 0 else TILES_PER_ROUND
+            step = 1 if r <= 1 else TILES_PER_ROUND
             for t in range(0, TILES_PER_ROUND, step):
                 nc.sync.dma_start(out=x_sb[:, t : t + step, :], in_=x_view[:, first + t : first + t + step, :])
             x_of[r] = x_sb
@@ -110,6 +110,8 @@ def tile_refattention_pa_t_kernel(
         nc.vector.memset(eps[:], EPS)
         ones = consts.tile([P, P], BF16)
         nc.vector.memset(ones[:], 1.0)
+        zeros = consts.tile([P, 4 * P], BF16)
+        nc.vector.memset(zeros[:], 0.0)
         table_warmer = consts.tile([P, 1], F32)
         nc.scalar.activation(out=table_warmer[:], in_=eps[:], func=ACT.Abs_reciprocal_sqrt)
 
@@ -159,7 +161,7 @@ def tile_refattention_pa_t_kernel(
                 (spread[:, 2, :], gain_rows[:, 1, :]),
             ):
                 nc.tensor.matmul(out=out, lhsT=ones[:], rhs=row, start=True, stop=True)
-            nc.vector.tensor_copy(out=gains[:], in_=spread[:, 0:3, :])
+            nc.scalar.copy(out=gains[:], in_=spread[:, 0:3, :])
 
         turned_of = {}
         grouped_of = {}
@@ -242,12 +244,17 @@ def tile_refattention_pa_t_kernel(
                         accum_out=sums[:, t, first_head + a : first_head + a + 1],
                     )
 
-        def reciprocal_rms(r):
-            rstd = stats.tile([P, TILES_PER_ROUND, HEADS], F32)
+        def reciprocal_rms(r, heads=slice(0, HEADS)):
+            if r not in rstd_of:
+                rstd = stats.tile([P, TILES_PER_ROUND, HEADS], F32)
+                rstd_of[r] = rstd
             nc.scalar.activation(
-                out=rstd[:], in_=sums_of[r][0][:], func=ACT.Abs_reciprocal_sqrt, scale=1.0 / D, bias=eps[:]
+                out=rstd_of[r][:, :, heads],
+                in_=sums_of[r][0][:, :, heads],
+                func=ACT.Abs_reciprocal_sqrt,
+                scale=1.0 / D,
+                bias=eps[:],
             )
-            rstd_of[r] = rstd
 
         def fold_tables(r):
             parts = work.tile([P, 2 * TILES_PER_ROUND + TILES_PER_ROUND * ROTATED // 2, D], F32)
@@ -297,20 +304,21 @@ def tile_refattention_pa_t_kernel(
             times(sin_low[:, :, 2, :], k_gained[:, :, high], tables[:, 1, tiles_of(r), low])
             times(sin_high[:, :, 2, :], k_gained[:, :, low], tables[:, 1, tiles_of(r), high])
 
-        def join(r):
+        def join_part(r, span, heads):
             folded, with_cos, sin_low, sin_high = work_of[r]
-            rotated = stats.tile([P, TILES_PER_ROUND, ROTATED, D], F32)
-            step = 1 if r == ROUNDS - 1 else TILES_PER_ROUND
-            for t in range(0, TILES_PER_ROUND, step):
-                span = slice(t, t + step)
-                for half, with_sin, op in ((low, sin_low, ALU.subtract), (high, sin_high[:], ALU.add)):
-                    nc.vector.tensor_tensor(
-                        out=rotated[:, span, :, half],
-                        in0=with_cos[:, span, :, half],
-                        in1=with_sin[:, span, :, :],
-                        op=op,
-                    )
-            rotated_of[r] = rotated
+            if r not in rotated_of:
+                rotated = stats.tile([P, TILES_PER_ROUND, ROTATED, D], F32)
+                rotated_of[r] = rotated
+            for half, with_sin, op in ((low, sin_low, ALU.subtract), (high, sin_high[:], ALU.add)):
+                nc.vector.tensor_tensor(
+                    out=rotated_of[r][:, span, heads, half],
+                    in0=with_cos[:, span, heads, half],
+                    in1=with_sin[:, span, heads, :],
+                    op=op,
+                )
+
+        def join(r):
+            join_part(r, slice(0, TILES_PER_ROUND), slice(0, ROTATED))
 
         def times_rstd_on_scalar(out, r, t, h):
             nc.scalar.activation(
@@ -336,20 +344,20 @@ def tile_refattention_pa_t_kernel(
                 times_rstd_on_vector(k_out[:, t, :], r, t, 2)
             nc.sync.dma_start(out=k_view[:, tiles_of(r), :], in_=k_out[:])
 
-        def finish_last(r):
+        def join_and_finish_last(r):
+            join_part(r, slice(0, TILES_PER_ROUND), slice(2, ROTATED))
+            join_part(r, slice(0, 1), slice(0, 2))
+            finish_k(r)
+            join_part(r, slice(1, 2), slice(0, 2))
             q_first = results.tile([P, 2, D], F32)
             q_head_0 = results.tile([P, D], F32)
             q_head_1 = results.tile([P, D], F32)
-            k_out = results.tile([P, TILES_PER_ROUND, D], F32)
             t0, t1 = r * TILES_PER_ROUND, r * TILES_PER_ROUND + 1
             for h in range(2):
                 times_rstd_on_scalar(q_first[:, h, :], r, 0, h)
             nc.sync.dma_start(out=q_view[:, :, t0, :], in_=q_first[:])
             times_rstd_on_scalar(q_head_0[:], r, 1, 0)
             nc.sync.dma_start(out=q_view[:, 0, t1, :], in_=q_head_0[:])
-            for t in range(TILES_PER_ROUND):
-                times_rstd_on_vector(k_out[:, t, :], r, t, 2)
-            nc.sync.dma_start(out=k_view[:, tiles_of(r), :], in_=k_out[:])
             times_rstd_on_vector(q_head_1[:], r, 1, 1)
             nc.sync.dma_start(out=q_view[:, 1, t1, :], in_=q_head_1[:])
 
@@ -367,13 +375,18 @@ def tile_refattention_pa_t_kernel(
         def in_range(r):
             return 0 <= r < ROUNDS
 
+        warm = psum_prod.tile([P, 2 * TILES_PER_ROUND, D], F32, tag="product_kv")
+        for n in range(5):
+            nc.tensor.matmul(
+                out=warm[:].rearrange("p n d -> p (n d)"), lhsT=ones[:], rhs=zeros[:], start=True, stop=True
+            )
         prepare_head(0)
         quantise_head(0)
         prepare_head(1)
         quantise_head(1)
         transpose_tokens(0)
-        spread_gains()
         regroup(0)
+        spread_gains()
         quantise(0, one_by_one)
         prepare_head(2)
         prepare_head(3)
@@ -418,23 +431,30 @@ def tile_refattention_pa_t_kernel(
             gain_k(i)
             multiply_q_sin(i, high)
             multiply_k(i)
+            q_out = results.tile([P, 2, TILES_PER_ROUND, D], F32)
             if in_range(i + 2):
                 regroup(i + 2)
-            q_out = results.tile([P, 2, TILES_PER_ROUND, D], F32)
-            if not in_range(i + 2):
+                sum_squares(i, 0)
+                finish_q(i - 1, 0, q_out)
+                reciprocal_rms(i)
+                finish_q(i - 1, 1, q_out)
+            elif in_range(i + 1):
                 finish_q(i - 1, 0, q_out)
                 finish_q(i - 1, 1, q_out)
                 sum_squares(i, 0)
                 reciprocal_rms(i)
             else:
-                sum_squares(i, 0)
+                reciprocal_rms(i, slice(2, HEADS))
                 finish_q(i - 1, 0, q_out)
-                reciprocal_rms(i)
                 finish_q(i - 1, 1, q_out)
+                finish_v(i)
+                sum_squares(i, 0)
+                reciprocal_rms(i, slice(0, 2))
             nc.sync.dma_start(out=q_view[:, :, tiles_of(i - 1), :], in_=q_out[:])
             finish_k(i - 1)
             if in_range(i + 2):
                 quantise(i + 2, together)
-            finish_v(i)
-            join(i)
-        finish_last(ROUNDS - 1)
+            if in_range(i + 1):
+                finish_v(i)
+                join(i)
+        join_and_finish_last(ROUNDS - 1)

@@ -34,6 +34,7 @@ ROUNDS = TILES // TILES_PER_ROUND
 LOAD_AHEAD = 6
 TABLE_SPLITS = (4, 12)
 
+COLUMN = (1, 2, 0, 3)
 FLOPS = 2 * TOKENS * HID * FEATURES
 
 
@@ -110,8 +111,6 @@ def tile_refattention_pa_t_kernel(
         nc.vector.memset(eps[:], EPS)
         ones = consts.tile([P, P], BF16)
         nc.vector.memset(ones[:], 1.0)
-        zeros = consts.tile([P, 4 * P], BF16)
-        nc.vector.memset(zeros[:], 0.0)
         table_warmer = consts.tile([P, 1], F32)
         nc.scalar.activation(out=table_warmer[:], in_=eps[:], func=ACT.Abs_reciprocal_sqrt)
 
@@ -228,33 +227,35 @@ def tile_refattention_pa_t_kernel(
         def project_kv(r):
             project(r, kv_of, 2)
 
-        def sum_squares(r, first_head):
+        def sum_squares(r, wanted):
             if r not in sums_of:
                 sums = stats.tile([P, TILES_PER_ROUND, HEADS], F32)
                 squares = stats.tile([P, TILES_PER_ROUND, HEADS, D], BF16)
                 sums_of[r] = (sums, squares)
             sums, squares = sums_of[r]
-            product = q_of[r] if first_head == 0 else kv_of[r]
-            for t in range(TILES_PER_ROUND):
-                for a in range(2):
-                    nc.scalar.activation(
-                        out=squares[:, t, first_head + a, :],
-                        in_=product[:, t, a, :],
-                        func=ACT.Square,
-                        accum_out=sums[:, t, first_head + a : first_head + a + 1],
-                    )
+            for t, h in wanted:
+                product = q_of[r] if h < 2 else kv_of[r]
+                nc.scalar.activation(
+                    out=squares[:, t, h, :],
+                    in_=product[:, t, h % 2, :],
+                    func=ACT.Square,
+                    accum_out=sums[:, t, COLUMN[h] : COLUMN[h] + 1],
+                )
 
-        def reciprocal_rms(r, heads=slice(0, HEADS)):
+        def reciprocal_rms(r, columns):
             if r not in rstd_of:
                 rstd = stats.tile([P, TILES_PER_ROUND, HEADS], F32)
                 rstd_of[r] = rstd
             nc.scalar.activation(
-                out=rstd_of[r][:, :, heads],
-                in_=sums_of[r][0][:, :, heads],
+                out=rstd_of[r][:, :, columns],
+                in_=sums_of[r][0][:, :, columns],
                 func=ACT.Abs_reciprocal_sqrt,
                 scale=1.0 / D,
                 bias=eps[:],
             )
+
+        def rstd_column(r, t, h):
+            return rstd_of[r][:, t, COLUMN[h] : COLUMN[h] + 1]
 
         def fold_tables(r):
             parts = work.tile([P, 2 * TILES_PER_ROUND + TILES_PER_ROUND * ROTATED // 2, D], F32)
@@ -294,7 +295,15 @@ def tile_refattention_pa_t_kernel(
 
         def gain_k(r):
             k_gained = stats.tile([P, TILES_PER_ROUND, D], F32)
-            times(k_gained[:], kv_of[r][:, :, 0, :], gains[:, 2, :].unsqueeze(1).to_broadcast([P, TILES_PER_ROUND, D]))
+            for t in range(TILES_PER_ROUND):
+                nc.vector.scalar_tensor_tensor(
+                    out=k_gained[:, t, :],
+                    in0=kv_of[r][:, t, 0, :],
+                    scalar=rstd_column(r, t, 2),
+                    in1=gains[:, 2, :],
+                    op0=ALU.mult,
+                    op1=ALU.mult,
+                )
             k_gained_of[r] = k_gained
 
         def multiply_k(r):
@@ -322,32 +331,25 @@ def tile_refattention_pa_t_kernel(
 
         def times_rstd_on_scalar(out, r, t, h):
             nc.scalar.activation(
-                out=out, in_=rotated_of[r][:, t, h, :], func=ACT.Copy, scale=rstd_of[r][:, t, h : h + 1]
+                out=out, in_=rotated_of[r][:, t, h, :], func=ACT.Copy, scale=rstd_column(r, t, h)
             )
 
         def times_rstd_on_vector(out, r, t, h):
             nc.vector.tensor_scalar(
                 out=out,
                 in0=rotated_of[r][:, t, h, :],
-                scalar1=rstd_of[r][:, t, h : h + 1],
+                scalar1=rstd_column(r, t, h),
                 scalar2=None,
                 op0=ALU.mult,
             )
 
-        def finish_q(r, t, q_out):
-            for h in range(2):
-                times_rstd_on_scalar(q_out[:, h, t, :], r, t, h)
-
-        def finish_k(r):
-            k_out = results.tile([P, TILES_PER_ROUND, D], F32)
-            for t in range(TILES_PER_ROUND):
-                times_rstd_on_vector(k_out[:, t, :], r, t, 2)
-            nc.sync.dma_start(out=k_view[:, tiles_of(r), :], in_=k_out[:])
+        def store_k(r):
+            nc.sync.dma_start(out=k_view[:, tiles_of(r), :], in_=rotated_of[r][:, :, 2, :])
 
         def join_and_finish_last(r):
             join_part(r, slice(0, TILES_PER_ROUND), slice(2, ROTATED))
+            store_k(r)
             join_part(r, slice(0, 1), slice(0, 2))
-            finish_k(r)
             join_part(r, slice(1, 2), slice(0, 2))
             q_first = results.tile([P, 2, D], F32)
             q_head_0 = results.tile([P, D], F32)
@@ -368,7 +370,7 @@ def tile_refattention_pa_t_kernel(
                     out=v_out[:, t, :],
                     in_=kv_of[r][:, t, 1, :],
                     func=ACT.Copy,
-                    scale=rstd_of[r][:, t, V_HEAD : V_HEAD + 1],
+                    scale=rstd_column(r, t, V_HEAD),
                 )
             nc.sync.dma_start(out=v_view[:, tiles_of(r), :], in_=v_out[:])
 
@@ -376,10 +378,8 @@ def tile_refattention_pa_t_kernel(
             return 0 <= r < ROUNDS
 
         warm = psum_prod.tile([P, 2 * TILES_PER_ROUND, D], F32, tag="product_kv")
-        for n in range(5):
-            nc.tensor.matmul(
-                out=warm[:].rearrange("p n d -> p (n d)"), lhsT=ones[:], rhs=zeros[:], start=True, stop=True
-            )
+        for n in range(16):
+            nc.tensor.matmul(out=warm[:, n % 4, :], lhsT=ones[:], rhs=ones[:], start=True, stop=True)
         prepare_head(0)
         quantise_head(0)
         prepare_head(1)
@@ -399,21 +399,24 @@ def tile_refattention_pa_t_kernel(
         regroup(1)
         multiply_q_sin(0, low)
         multiply_q_sin(0, high)
-        sum_squares(0, 0)
         project_kv(0)
-        gain_k(0)
-        sum_squares(0, 2)
+        sum_squares(0, ((0, 2), (1, 2), (0, 3)))
+        reciprocal_rms(0, slice(0, 1))
+        sum_squares(0, ((1, 3),))
         transpose_tokens(2)
         quantise(1, together)
+        gain_k(0)
+        sum_squares(0, ((0, 0), (0, 1), (1, 0), (1, 1)))
         project_q(1)
         project_kv(1)
         fold_tables(1)
-        multiply_k(0)
         regroup(2)
         transpose_tokens(3)
-        reciprocal_rms(0)
+        reciprocal_rms(0, slice(1, HEADS))
         finish_v(0)
+        multiply_k(0)
         join(0)
+        store_k(0)
         quantise(2, together)
 
         for i in range(1, ROUNDS):
@@ -425,7 +428,8 @@ def tile_refattention_pa_t_kernel(
                 fold_tables(i + 1)
             if in_range(i + 3):
                 transpose_tokens(i + 3)
-            sum_squares(i, 2)
+            sum_squares(i, ((0, 2), (1, 2), (0, 3), (1, 3)))
+            reciprocal_rms(i, slice(0, 1))
             multiply_q_cos(i)
             multiply_q_sin(i, low)
             gain_k(i)
@@ -434,27 +438,23 @@ def tile_refattention_pa_t_kernel(
             q_out = results.tile([P, 2, TILES_PER_ROUND, D], F32)
             if in_range(i + 2):
                 regroup(i + 2)
-                sum_squares(i, 0)
-                finish_q(i - 1, 0, q_out)
-                reciprocal_rms(i)
-                finish_q(i - 1, 1, q_out)
-            elif in_range(i + 1):
-                finish_q(i - 1, 0, q_out)
-                finish_q(i - 1, 1, q_out)
-                sum_squares(i, 0)
-                reciprocal_rms(i)
+                sum_squares(i, ((0, 0), (0, 1), (1, 0), (1, 1)))
+                times_rstd_on_scalar(q_out[:, 0, 0, :], i - 1, 0, 0)
+                times_rstd_on_scalar(q_out[:, 1, 0, :], i - 1, 0, 1)
+                reciprocal_rms(i, slice(1, HEADS))
+                times_rstd_on_scalar(q_out[:, 0, 1, :], i - 1, 1, 0)
             else:
-                reciprocal_rms(i, slice(2, HEADS))
-                finish_q(i - 1, 0, q_out)
-                finish_q(i - 1, 1, q_out)
-                finish_v(i)
-                sum_squares(i, 0)
-                reciprocal_rms(i, slice(0, 2))
+                times_rstd_on_scalar(q_out[:, 0, 0, :], i - 1, 0, 0)
+                times_rstd_on_scalar(q_out[:, 1, 0, :], i - 1, 0, 1)
+                times_rstd_on_scalar(q_out[:, 0, 1, :], i - 1, 1, 0)
+                sum_squares(i, ((0, 0), (0, 1), (1, 0), (1, 1)))
+                reciprocal_rms(i, slice(1, HEADS))
+            times_rstd_on_vector(q_out[:, 1, 1, :], i - 1, 1, 1)
             nc.sync.dma_start(out=q_view[:, :, tiles_of(i - 1), :], in_=q_out[:])
-            finish_k(i - 1)
             if in_range(i + 2):
                 quantise(i + 2, together)
+            finish_v(i)
             if in_range(i + 1):
-                finish_v(i)
                 join(i)
+                store_k(i)
         join_and_finish_last(ROUNDS - 1)

@@ -443,18 +443,26 @@ def tile_refattention_pa_t_kernel(
                 times_rstd_on_scalar(q_out[:, 1, 0, :], i - 1, 0, 1)
                 reciprocal_rms(i, slice(1, HEADS))
                 times_rstd_on_scalar(q_out[:, 0, 1, :], i - 1, 1, 0)
-            else:
-                times_rstd_on_scalar(q_out[:, 0, 0, :], i - 1, 0, 0)
-                times_rstd_on_scalar(q_out[:, 1, 0, :], i - 1, 0, 1)
-                times_rstd_on_scalar(q_out[:, 0, 1, :], i - 1, 1, 0)
+                times_rstd_on_vector(q_out[:, 1, 1, :], i - 1, 1, 1)
+            elif in_range(i + 1):
+                for t in range(TILES_PER_ROUND):
+                    for h in range(2):
+                        times_rstd_on_scalar(q_out[:, h, t, :], i - 1, t, h)
                 sum_squares(i, ((0, 0), (0, 1), (1, 0), (1, 1)))
                 reciprocal_rms(i, slice(1, HEADS))
-            times_rstd_on_vector(q_out[:, 1, 1, :], i - 1, 1, 1)
+            else:
+                reciprocal_rms(i, slice(3, HEADS))
+                for t in range(TILES_PER_ROUND):
+                    for h in range(2):
+                        times_rstd_on_scalar(q_out[:, h, t, :], i - 1, t, h)
+                finish_v(i)
+                sum_squares(i, ((0, 0), (0, 1), (1, 0), (1, 1)))
+                reciprocal_rms(i, slice(1, 3))
             nc.sync.dma_start(out=q_view[:, :, tiles_of(i - 1), :], in_=q_out[:])
             if in_range(i + 2):
                 quantise(i + 2, together)
-            finish_v(i)
             if in_range(i + 1):
+                finish_v(i)
                 join(i)
                 store_k(i)
         join_and_finish_last(ROUNDS - 1)

@@ -29,12 +29,11 @@ PASSES = HID // K_PASS
 WORDS = HID // 2
 TURNS = WORDS // P
 TILES = TOKENS // P
-TILES_PER_ROUND = 2
-ROUNDS = TILES // TILES_PER_ROUND
-LOAD_AHEAD = 6
+T = 2
+ROUNDS = TILES // T
+LOAD_AHEAD = 7
 TABLE_SPLITS = (4, 12)
 
-COLUMN = (1, 2, 0, 3)
 FLOPS = 2 * TOKENS * HID * FEATURES
 
 
@@ -55,12 +54,12 @@ def tile_refattention_pa_t_kernel(
         consts = stack.enter_context(tc.tile_pool(name="consts", bufs=1))
         x_pool = stack.enter_context(tc.tile_pool(name="x", bufs=ROUNDS))
         w_pool = stack.enter_context(tc.tile_pool(name="w", bufs=HEADS))
-        stage = stack.enter_context(tc.tile_pool(name="stage", bufs=2))
+        stage = stack.enter_context(tc.tile_pool(name="stage", bufs=3))
         stats = stack.enter_context(tc.tile_pool(name="stats", bufs=3))
-        results = stack.enter_context(tc.tile_pool(name="results", bufs=3))
-        work = stack.enter_context(tc.tile_pool(name="work", bufs=2))
-        psum_turn = stack.enter_context(tc.psum_pool(name="psum_turn", bufs=2 * TILES_PER_ROUND))
-        psum_prod = stack.enter_context(tc.psum_pool(name="psum_prod", bufs=2))
+        work = stack.enter_context(tc.tile_pool(name="work", bufs=3))
+        psum_turn = stack.enter_context(tc.psum_pool(name="psum_turn", bufs=3))
+        psum_prod = stack.enter_context(tc.psum_pool(name="psum_prod", bufs=4))
+        psum_table = stack.enter_context(tc.psum_pool(name="psum_table", bufs=1))
 
         identity = consts.tile([P, P], F32)
         make_identity(nc, identity[:])
@@ -76,13 +75,14 @@ def tile_refattention_pa_t_kernel(
 
         x_of = {}
 
-        def load_tokens(r):
-            x_sb = x_pool.tile([P, TILES_PER_ROUND, HID], BF16)
-            first = r * TILES_PER_ROUND
-            step = 1 if r <= 1 else TILES_PER_ROUND
-            for t in range(0, TILES_PER_ROUND, step):
-                nc.sync.dma_start(out=x_sb[:, t : t + step, :], in_=x_view[:, first + t : first + t + step, :])
-            x_of[r] = x_sb
+        def load_tokens(r, tiles):
+            if r not in x_of:
+                x_sb = x_pool.tile([P, T, HID], BF16)
+                x_of[r] = x_sb
+            first = r * T
+            nc.sync.dma_start(
+                out=x_of[r][:, tiles, :], in_=x_view[:, first + tiles.start : first + tiles.stop, :]
+            )
 
         tables = consts.tile([P, 2, TILES, D], BF16)
 
@@ -90,52 +90,69 @@ def tile_refattention_pa_t_kernel(
             for a, view in enumerate((cos_view, sin_view)):
                 nc.sync.dma_start(out=tables[:, a, first:last, :], in_=view[:, first:last, :])
 
+        both_tiles = slice(0, T)
+        load_tokens(0, slice(0, 1))
         load_head(0)
         load_head(1)
         for a, w in enumerate((q_norm_w, k_norm_w)):
             nc.sync.dma_start(out=gain_rows[0:1, a, :], in_=w.rearrange("(o d) -> o d", o=1))
-        load_tokens(0)
         load_head(2)
         load_head(3)
+        load_tokens(0, slice(1, 2))
+        load_tokens(1, slice(0, 1))
+        load_tokens(1, slice(1, 2))
         load_tables(0, TABLE_SPLITS[0])
-        load_tokens(1)
-        load_tokens(2)
+        load_tokens(2, both_tiles)
+        load_tokens(3, both_tiles)
         load_tables(TABLE_SPLITS[0], TABLE_SPLITS[1])
-        load_tokens(3)
+        load_tokens(4, both_tiles)
+        load_tokens(5, both_tiles)
         load_tables(TABLE_SPLITS[1], TILES)
-        load_tokens(4)
-        load_tokens(5)
-        load_tokens(6)
+        load_tokens(6, both_tiles)
 
-        eps = consts.tile([P, 1], F32)
-        nc.vector.memset(eps[:], EPS)
         ones = consts.tile([P, P], BF16)
         nc.vector.memset(ones[:], 1.0)
+        eps = consts.tile([P, 1], F32)
+        nc.vector.memset(eps[:], EPS)
         table_warmer = consts.tile([P, 1], F32)
         nc.scalar.activation(out=table_warmer[:], in_=eps[:], func=ACT.Abs_reciprocal_sqrt)
+        plus_identity = consts.tile([P, P], BF16)
+        minus_identity = consts.tile([P, P], BF16)
+        nc.vector.tensor_copy(out=plus_identity[:], in_=identity[:])
+        nc.vector.tensor_scalar(
+            out=minus_identity[:], in0=identity[:], scalar1=-1.0, scalar2=None, op0=ALU.mult
+        )
 
-        def turn(rows_as_words):
-            turned = psum_turn.tile([P, TURNS, P], F32)
+        def turn(turned, rows_as_words):
             for c in range(TURNS):
                 g, u = divmod(c, 2)
                 every_second = rows_as_words[:, 2 * P * g + u : 2 * P * (g + 1) : 2]
                 nc.tensor.transpose(turned[:, c, :], every_second, identity[:])
-            return turned
 
         def side_by_side(turned):
             return turned[:].rearrange("p (g u) r -> p g r u", u=2)
 
+        def copy_on(engine, out, in_):
+            if engine is nc.scalar:
+                nc.scalar.copy(out=out, in_=in_)
+            else:
+                nc.vector.tensor_copy(out=out, in_=in_)
+
         w_words = w_raw[:].bitcast(F32)
         w_codes = consts.tile([P, PASSES, FEATURES], U32, align_bytes=64)
         w_scales = consts.tile([P, PASSES, FEATURES], U8, align_bytes=64)
-
+        w_turned_of = {}
         w_grouped_of = {}
 
-        def prepare_head(h):
-            turned = turn(w_words[:, h, :])
+        def turn_head(h):
+            turned = psum_prod.tile([P, TURNS, P], F32, tag="product")
+            turn(turned, w_words[:, h, :])
+            w_turned_of[h] = turned
+
+        def regroup_head(h, engine):
             w_grouped = w_pool.tile([P, PASSES, D, PACK], BF16, align_bytes=64)
             w_grouped_of[h] = w_grouped
-            nc.scalar.copy(out=w_grouped[:].bitcast(F32), in_=side_by_side(turned))
+            copy_on(engine, w_grouped[:].bitcast(F32), side_by_side(w_turned_of[h]))
 
         def quantise_head(h):
             columns = slice(h * D, (h + 1) * D)
@@ -146,323 +163,291 @@ def tile_refattention_pa_t_kernel(
                     in_=w_grouped_of[h][:, g, :, :].rearrange("p f t -> p (f t)"),
                 )
 
-
         low = slice(0, HALF)
         high = slice(HALF, D)
-        gains = consts.tile([P, 3, D], BF16)
+        gains = consts.tile([P, 2, D], BF16)
 
         def spread_gains():
-            spread = psum_prod.tile([P, 2 * TILES_PER_ROUND, D], F32, tag="product_kv")
-            for out, row in (
-                (spread[:, 0, :], gain_rows[:, 0, :]),
-                (spread[:, 1, low], gain_rows[:, 0, high]),
-                (spread[:, 1, high], gain_rows[:, 0, low]),
-                (spread[:, 2, :], gain_rows[:, 1, :]),
-            ):
-                nc.tensor.matmul(out=out, lhsT=ones[:], rhs=row, start=True, stop=True)
-            nc.scalar.copy(out=gains[:], in_=spread[:, 0:3, :])
+            bank = psum_table.tile([P, 4, D], F32)
+            nc.tensor.matmul(
+                out=bank[:, 0:2, :].rearrange("p a d -> p (a d)"),
+                lhsT=ones[:],
+                rhs=gain_rows[:].rearrange("p a d -> p (a d)"),
+                start=True,
+                stop=True,
+            )
+            nc.scalar.copy(out=gains[:], in_=bank[:, 0:2, :])
 
         turned_of = {}
         grouped_of = {}
         codes_of = {}
-        q_of = {}
-        kv_of = {}
+        product_of = {}
         sums_of = {}
         rstd_of = {}
+        table_of = {}
+        gained_of = {}
         work_of = {}
-        k_gained_of = {}
-        rotated_of = {}
+        v_of = {}
 
         def tiles_of(r):
-            first = r * TILES_PER_ROUND
-            return slice(first, first + TILES_PER_ROUND)
+            return slice(r * T, (r + 1) * T)
 
-        def transpose_tokens(r):
-            x_words = x_of[r][:].bitcast(F32)
-            turned_of[r] = [turn(x_words[:, t, :]) for t in range(TILES_PER_ROUND)]
+        def transpose_tile(r, t):
+            turned = psum_turn.tile([P, TURNS, P], F32)
+            turn(turned, x_of[r][:].bitcast(F32)[:, t, :])
+            turned_of[r, t] = turned
 
-        def regroup(r):
-            grouped = stage.tile([P, TILES_PER_ROUND, PASSES, P, PACK], BF16, align_bytes=64)
-            grouped_words = grouped[:].bitcast(F32)
-            for t in range(TILES_PER_ROUND):
-                nc.scalar.copy(out=grouped_words[:, t], in_=side_by_side(turned_of[r][t]))
-            grouped_of[r] = grouped
+        def regroup(r, t, engine):
+            if r not in grouped_of:
+                grouped = stage.tile([P, T, PASSES, P, PACK], BF16, align_bytes=64)
+                grouped_of[r] = grouped
+            words = grouped_of[r][:].bitcast(F32)
+            copy_on(engine, words[:, t], side_by_side(turned_of[r, t]))
 
-        def quantise(r, spans):
-            for span in spans:
-                if r not in codes_of:
-                    codes = stats.tile([P, TILES_PER_ROUND, PASSES, P], U32, align_bytes=64)
-                    scales = stats.tile([P, TILES_PER_ROUND, PASSES, P], U8, align_bytes=64)
-                    codes_of[r] = (codes, scales)
-                codes, scales = codes_of[r]
-                nc.vector.quantize_mx(
-                    out=codes[:, span].rearrange("p t g r -> p (t g r)").bitcast(FP8X4),
-                    scales=scales[:, span].rearrange("p t g r -> p (t g r)"),
-                    in_=grouped_of[r][:, span].rearrange("p t g r v -> p (t g r v)"),
+        def quantise(r, span):
+            if r not in codes_of:
+                codes = stage.tile([P, T, PASSES, P], U32, align_bytes=64)
+                scales = stage.tile([P, T, PASSES, P], U8, align_bytes=64)
+                codes_of[r] = (codes, scales)
+            codes, scales = codes_of[r]
+            nc.vector.quantize_mx(
+                out=codes[:, span].rearrange("p t g r -> p (t g r)").bitcast(FP8X4),
+                scales=scales[:, span].rearrange("p t g r -> p (t g r)"),
+                in_=grouped_of[r][:, span].rearrange("p t g r v -> p (t g r v)"),
+            )
+
+        def project(r, t, heads):
+            codes, scales = codes_of[r]
+            if (r, t) not in product_of:
+                product = psum_prod.tile([P, HEADS, D], F32, tag="product")
+                product_of[r, t] = product
+            columns = slice(heads.start * D, heads.stop * D)
+            for g in range(PASSES):
+                nc.tensor.matmul_mx(
+                    out=product_of[r, t][:, heads, :].rearrange("p h d -> p (h d)"),
+                    lhsT=codes[:, t, g, :].bitcast(FP8X4),
+                    lhsT_scale=scales[:, t, g, :],
+                    rhs=w_codes[:, g, columns].bitcast(FP8X4),
+                    rhs_scale=w_scales[:, g, columns],
+                    start=(g == 0),
+                    stop=(g == PASSES - 1),
                 )
 
-        one_by_one = [slice(t, t + 1) for t in range(TILES_PER_ROUND)]
-        together = [slice(0, TILES_PER_ROUND)]
+        all_heads = slice(0, HEADS)
 
-        def project(r, of, first):
-            codes, scales = codes_of[r]
-            product = psum_prod.tile([P, TILES_PER_ROUND * 2, D], F32, tag="product_q" if first == 0 else "product_kv")
-            columns = slice(first * D, (first + 2) * D)
-            for t in range(TILES_PER_ROUND):
-                for g in range(PASSES):
-                    nc.tensor.matmul_mx(
-                        out=product[:, 2 * t : 2 * t + 2, :].rearrange("p h d -> p (h d)"),
-                        lhsT=codes[:, t, g, :].bitcast(FP8X4),
-                        lhsT_scale=scales[:, t, g, :],
-                        rhs=w_codes[:, g, columns].bitcast(FP8X4),
-                        rhs_scale=w_scales[:, g, columns],
-                        start=(g == 0),
-                        stop=(g == PASSES - 1),
-                    )
-            of[r] = product[:].rearrange("p (t h) d -> p t h d", h=2)
-
-        def project_q(r):
-            project(r, q_of, 0)
-
-        def project_kv(r):
-            project(r, kv_of, 2)
-
-        def sum_squares(r, wanted):
+        def sum_squares(r, t, heads):
             if r not in sums_of:
-                sums = stats.tile([P, TILES_PER_ROUND, HEADS], F32)
-                squares = stats.tile([P, TILES_PER_ROUND, HEADS, D], BF16)
+                sums = stats.tile([P, T, HEADS], F32)
+                squares = stats.tile([P, T, HEADS, D], BF16)
                 sums_of[r] = (sums, squares)
             sums, squares = sums_of[r]
-            for t, h in wanted:
-                product = q_of[r] if h < 2 else kv_of[r]
+            for h in range(heads.start, heads.stop):
                 nc.scalar.activation(
                     out=squares[:, t, h, :],
-                    in_=product[:, t, h % 2, :],
+                    in_=product_of[r, t][:, h, :],
                     func=ACT.Square,
-                    accum_out=sums[:, t, COLUMN[h] : COLUMN[h] + 1],
+                    accum_out=sums[:, t, h : h + 1],
                 )
 
-        def reciprocal_rms(r, columns):
+        def reciprocal_rms(r, span):
             if r not in rstd_of:
-                rstd = stats.tile([P, TILES_PER_ROUND, HEADS], F32)
+                rstd = stats.tile([P, T, HEADS], F32)
                 rstd_of[r] = rstd
             nc.scalar.activation(
-                out=rstd_of[r][:, :, columns],
-                in_=sums_of[r][0][:, :, columns],
+                out=rstd_of[r][:, span, :],
+                in_=sums_of[r][0][:, span, :],
                 func=ACT.Abs_reciprocal_sqrt,
                 scale=1.0 / D,
                 bias=eps[:],
             )
 
-        def rstd_column(r, t, h):
-            return rstd_of[r][:, t, COLUMN[h] : COLUMN[h] + 1]
+        def finish_v(r, t):
+            if r not in v_of:
+                v_out = stats.tile([P, T, D], F32)
+                v_of[r] = v_out
+            nc.scalar.activation(
+                out=v_of[r][:, t, :],
+                in_=product_of[r, t][:, V_HEAD, :],
+                func=ACT.Copy,
+                scale=rstd_of[r][:, t, V_HEAD : V_HEAD + 1],
+            )
+            if t == T - 1:
+                nc.sync.dma_start(out=v_view[:, tiles_of(r), :], in_=v_of[r][:])
 
-        def fold_tables(r):
-            parts = work.tile([P, 2 * TILES_PER_ROUND + TILES_PER_ROUND * ROTATED // 2, D], F32)
-            folded = parts[:, 0 : 2 * TILES_PER_ROUND, :].rearrange("p (a t) d -> p a t d", a=2)
-            engine = nc.vector if r == 0 else nc.gpsimd
-            engine.tensor_tensor(
-                out=folded,
-                in0=tables[:, :, tiles_of(r), :],
-                in1=gains[:, 0:2, :].unsqueeze(2).to_broadcast([P, 2, TILES_PER_ROUND, D]),
-                op=ALU.mult,
-            )
-            sin_low = (
-                parts[:, 2 * TILES_PER_ROUND :, :]
-                .rearrange("p n d -> p (n d)")
-                .rearrange("p (t h d) -> p t h d", h=ROTATED, d=HALF)
-            )
-            sin_high = work.tile([P, TILES_PER_ROUND, ROTATED, HALF], F32)
-            with_cos = work.tile([P, TILES_PER_ROUND, ROTATED, D], F32)
-            work_of[r] = (folded, with_cos, sin_low, sin_high)
+        def bring_tables(r):
+            bank = psum_table.tile([P, 4, D], F32)
+            table_of[r] = bank
+            for out, sign, rows in (
+                (bank[:, 0:2, :], plus_identity, tables[:, 0, tiles_of(r), :]),
+                (bank[:, 2, :].rearrange("p (t d) -> p t d", t=T), minus_identity, tables[:, 1, tiles_of(r), low]),
+                (bank[:, 3, :].rearrange("p (t d) -> p t d", t=T), plus_identity, tables[:, 1, tiles_of(r), high]),
+            ):
+                nc.tensor.matmul(out=out, lhsT=sign[:], rhs=rows, start=True, stop=True)
+
+        def gain(r, t):
+            if r not in gained_of:
+                gained = work.tile([P, ROTATED, T, D], F32)
+                gained_of[r] = gained
+            for h in ((0, 1, 2) if t == 0 else (2, 0, 1)):
+                nc.vector.scalar_tensor_tensor(
+                    out=gained_of[r][:, h, t, :],
+                    in0=product_of[r, t][:, h, :],
+                    scalar=rstd_of[r][:, t, h : h + 1],
+                    in1=gains[:, h // 2, :],
+                    op0=ALU.mult,
+                    op1=ALU.mult,
+                )
 
         def times(out, in0, in1):
             nc.vector.tensor_tensor(out=out, in0=in0, in1=in1, op=ALU.mult)
 
-        def both(table):
-            return table.unsqueeze(2).to_broadcast([P, TILES_PER_ROUND, 2, table.shape[-1]])
+        def parts_of(r):
+            if r not in work_of:
+                with_cos = work.tile([P, ROTATED, T, D], F32)
+                with_sin = work.tile([P, ROTATED, T, D], F32)
+                rotated = work.tile([P, ROTATED, T, D], F32)
+                work_of[r] = (with_cos, with_sin, rotated)
+            return work_of[r]
 
-        def multiply_q_cos(r):
-            folded, with_cos, sin_low, sin_high = work_of[r]
-            times(with_cos[:, :, 0:2, :], q_of[r], both(folded[:, 0, :, :]))
-
-        def multiply_q_sin(r, half):
-            folded, with_cos, sin_low, sin_high = work_of[r]
-            if half == low:
-                times(sin_low[:, :, 0:2, :], q_of[r][:, :, :, high], both(folded[:, 1, :, low]))
-            else:
-                times(sin_high[:, :, 0:2, :], q_of[r][:, :, :, low], both(folded[:, 1, :, high]))
-
-        def gain_k(r):
-            k_gained = stats.tile([P, TILES_PER_ROUND, D], F32)
-            for t in range(TILES_PER_ROUND):
-                nc.vector.scalar_tensor_tensor(
-                    out=k_gained[:, t, :],
-                    in0=kv_of[r][:, t, 0, :],
-                    scalar=rstd_column(r, t, 2),
-                    in1=gains[:, 2, :],
-                    op0=ALU.mult,
-                    op1=ALU.mult,
-                )
-            k_gained_of[r] = k_gained
-
-        def multiply_k(r):
-            folded, with_cos, sin_low, sin_high = work_of[r]
-            k_gained = k_gained_of[r]
-            times(with_cos[:, :, 2, :], k_gained[:], tables[:, 0, tiles_of(r), :])
-            times(sin_low[:, :, 2, :], k_gained[:, :, high], tables[:, 1, tiles_of(r), low])
-            times(sin_high[:, :, 2, :], k_gained[:, :, low], tables[:, 1, tiles_of(r), high])
-
-        def join_part(r, span, heads):
-            folded, with_cos, sin_low, sin_high = work_of[r]
-            if r not in rotated_of:
-                rotated = stats.tile([P, TILES_PER_ROUND, ROTATED, D], F32)
-                rotated_of[r] = rotated
-            for half, with_sin, op in ((low, sin_low, ALU.subtract), (high, sin_high[:], ALU.add)):
-                nc.vector.tensor_tensor(
-                    out=rotated_of[r][:, span, heads, half],
-                    in0=with_cos[:, span, heads, half],
-                    in1=with_sin[:, span, heads, :],
-                    op=op,
-                )
-
-        def join(r):
-            join_part(r, slice(0, TILES_PER_ROUND), slice(0, ROTATED))
-
-        def times_rstd_on_scalar(out, r, t, h):
-            nc.scalar.activation(
-                out=out, in_=rotated_of[r][:, t, h, :], func=ACT.Copy, scale=rstd_column(r, t, h)
+        def rotate_cos(r, heads):
+            with_cos, with_sin, rotated = parts_of(r)
+            n = heads.stop - heads.start
+            times(
+                with_cos[:, heads],
+                gained_of[r][:, heads],
+                table_of[r][:, 0:2, :].unsqueeze(1).to_broadcast([P, n, T, D]),
             )
 
-        def times_rstd_on_vector(out, r, t, h):
-            nc.vector.tensor_scalar(
-                out=out,
-                in0=rotated_of[r][:, t, h, :],
-                scalar1=rstd_column(r, t, h),
-                scalar2=None,
-                op0=ALU.mult,
+        def rotate_sin(r, heads):
+            with_cos, with_sin, rotated = parts_of(r)
+            n = heads.stop - heads.start
+            for a, half, other in ((2, low, high), (3, high, low)):
+                half_table = table_of[r][:, a, :].rearrange("p (t d) -> p t d", t=T)
+                times(
+                    with_sin[:, heads, :, half],
+                    gained_of[r][:, heads, :, other],
+                    half_table.unsqueeze(1).to_broadcast([P, n, T, HALF]),
+                )
+
+        rotated_heads = slice(0, ROTATED)
+
+        def join(r, engine, heads, span):
+            with_cos, with_sin, rotated = parts_of(r)
+            engine.tensor_tensor(
+                out=rotated[:, heads, span],
+                in0=with_cos[:, heads, span],
+                in1=with_sin[:, heads, span],
+                op=ALU.add,
             )
 
         def store_k(r):
-            nc.sync.dma_start(out=k_view[:, tiles_of(r), :], in_=rotated_of[r][:, :, 2, :])
+            nc.sync.dma_start(out=k_view[:, tiles_of(r), :], in_=work_of[r][2][:, 2])
 
-        def join_and_finish_last(r):
-            join_part(r, slice(0, TILES_PER_ROUND), slice(2, ROTATED))
-            store_k(r)
-            join_part(r, slice(0, 1), slice(0, 2))
-            join_part(r, slice(1, 2), slice(0, 2))
-            q_first = results.tile([P, 2, D], F32)
-            q_head_0 = results.tile([P, D], F32)
-            q_head_1 = results.tile([P, D], F32)
-            t0, t1 = r * TILES_PER_ROUND, r * TILES_PER_ROUND + 1
-            for h in range(2):
-                times_rstd_on_scalar(q_first[:, h, :], r, 0, h)
-            nc.sync.dma_start(out=q_view[:, :, t0, :], in_=q_first[:])
-            times_rstd_on_scalar(q_head_0[:], r, 1, 0)
-            nc.sync.dma_start(out=q_view[:, 0, t1, :], in_=q_head_0[:])
-            times_rstd_on_vector(q_head_1[:], r, 1, 1)
-            nc.sync.dma_start(out=q_view[:, 1, t1, :], in_=q_head_1[:])
-
-        def finish_v(r):
-            v_out = results.tile([P, TILES_PER_ROUND, D], F32)
-            for t in range(TILES_PER_ROUND):
-                nc.scalar.activation(
-                    out=v_out[:, t, :],
-                    in_=kv_of[r][:, t, 1, :],
-                    func=ACT.Copy,
-                    scale=rstd_column(r, t, V_HEAD),
-                )
-            nc.sync.dma_start(out=v_view[:, tiles_of(r), :], in_=v_out[:])
+        warm = psum_prod.tile([P, HEADS, D], F32, tag="product")
+        for n in range(16):
+            nc.tensor.matmul(out=warm[:, n % HEADS, :], lhsT=ones[:], rhs=ones[:], start=True, stop=True)
+        S, V = nc.scalar, nc.vector
+        transpose_tile(0, 0)
+        regroup(0, 0, S)
+        quantise(0, slice(0, 1))
+        turn_head(0)
+        regroup_head(0, S)
+        turn_head(1)
+        regroup_head(1, V)
+        quantise_head(0)
+        quantise_head(1)
+        turn_head(2)
+        regroup_head(2, S)
+        quantise_head(2)
+        turn_head(3)
+        regroup_head(3, S)
+        quantise_head(3)
+        project(0, 0, slice(0, 2))
+        sum_squares(0, 0, slice(0, 2))
+        transpose_tile(0, 1)
+        regroup(0, 1, V)
+        spread_gains()
+        project(0, 0, slice(2, 4))
+        sum_squares(0, 0, slice(2, 4))
+        quantise(0, slice(1, 2))
+        reciprocal_rms(0, slice(0, 1))
+        transpose_tile(1, 0)
+        project(0, 1, all_heads)
+        bring_tables(0)
+        gain(0, 0)
+        transpose_tile(1, 1)
+        regroup(1, 0, V)
+        sum_squares(0, 1, all_heads)
+        reciprocal_rms(0, slice(1, 2))
+        regroup(1, 1, S)
+        gain(0, 1)
+        quantise(1, both_tiles)
+        transpose_tile(2, 0)
+        regroup(2, 0, S)
+        transpose_tile(2, 1)
+        project(1, 0, all_heads)
+        project(1, 1, all_heads)
+        regroup(2, 1, S)
+        for t in range(T):
+            finish_v(0, t)
+            transpose_tile(3, t)
+        rotate_cos(0, rotated_heads)
+        rotate_sin(0, rotated_heads)
+        quantise(2, both_tiles)
 
         def in_range(r):
-            return 0 <= r < ROUNDS
+            return r < ROUNDS
 
-        warm = psum_prod.tile([P, 2 * TILES_PER_ROUND, D], F32, tag="product_kv")
-        for n in range(16):
-            nc.tensor.matmul(out=warm[:, n % 4, :], lhsT=ones[:], rhs=ones[:], start=True, stop=True)
-        prepare_head(0)
-        quantise_head(0)
-        prepare_head(1)
-        quantise_head(1)
-        transpose_tokens(0)
-        regroup(0)
-        spread_gains()
-        quantise(0, one_by_one)
-        prepare_head(2)
-        prepare_head(3)
-        project_q(0)
-        fold_tables(0)
-        quantise_head(2)
-        multiply_q_cos(0)
-        quantise_head(3)
-        transpose_tokens(1)
-        regroup(1)
-        multiply_q_sin(0, low)
-        multiply_q_sin(0, high)
-        project_kv(0)
-        sum_squares(0, ((0, 2), (1, 2), (0, 3)))
-        reciprocal_rms(0, slice(0, 1))
-        sum_squares(0, ((1, 3),))
-        transpose_tokens(2)
-        quantise(1, together)
-        gain_k(0)
-        sum_squares(0, ((0, 0), (0, 1), (1, 0), (1, 1)))
-        project_q(1)
-        project_kv(1)
-        fold_tables(1)
-        regroup(2)
-        transpose_tokens(3)
-        reciprocal_rms(0, slice(1, HEADS))
-        finish_v(0)
-        multiply_k(0)
-        join(0)
-        store_k(0)
-        quantise(2, together)
-
-        for i in range(1, ROUNDS):
+        for i in range(ROUNDS):
             if in_range(i + LOAD_AHEAD):
-                load_tokens(i + LOAD_AHEAD)
-            if in_range(i + 1):
-                project_q(i + 1)
-                project_kv(i + 1)
-                fold_tables(i + 1)
-            if in_range(i + 3):
-                transpose_tokens(i + 3)
-            sum_squares(i, ((0, 2), (1, 2), (0, 3), (1, 3)))
-            reciprocal_rms(i, slice(0, 1))
-            multiply_q_cos(i)
-            multiply_q_sin(i, low)
-            gain_k(i)
-            multiply_q_sin(i, high)
-            multiply_k(i)
-            q_out = results.tile([P, 2, TILES_PER_ROUND, D], F32)
+                load_tokens(i + LOAD_AHEAD, both_tiles)
+            if i > 0:
+                for t in range(T):
+                    gain(i, t)
+            if i == 1:
+                quantise(3, both_tiles)
             if in_range(i + 2):
-                regroup(i + 2)
-                sum_squares(i, ((0, 0), (0, 1), (1, 0), (1, 1)))
-                times_rstd_on_scalar(q_out[:, 0, 0, :], i - 1, 0, 0)
-                times_rstd_on_scalar(q_out[:, 1, 0, :], i - 1, 0, 1)
-                reciprocal_rms(i, slice(1, HEADS))
-                times_rstd_on_scalar(q_out[:, 0, 1, :], i - 1, 1, 0)
-                times_rstd_on_vector(q_out[:, 1, 1, :], i - 1, 1, 1)
-            elif in_range(i + 1):
-                for t in range(TILES_PER_ROUND):
-                    for h in range(2):
-                        times_rstd_on_scalar(q_out[:, h, t, :], i - 1, t, h)
-                sum_squares(i, ((0, 0), (0, 1), (1, 0), (1, 1)))
-                reciprocal_rms(i, slice(1, HEADS))
-            else:
-                reciprocal_rms(i, slice(3, HEADS))
-                for t in range(TILES_PER_ROUND):
-                    for h in range(2):
-                        times_rstd_on_scalar(q_out[:, h, t, :], i - 1, t, h)
-                finish_v(i)
-                sum_squares(i, ((0, 0), (0, 1), (1, 0), (1, 1)))
-                reciprocal_rms(i, slice(1, 3))
-            nc.sync.dma_start(out=q_view[:, :, tiles_of(i - 1), :], in_=q_out[:])
-            if in_range(i + 2):
-                quantise(i + 2, together)
+                for t in range(T):
+                    project(i + 2, t, all_heads)
             if in_range(i + 1):
-                finish_v(i)
-                join(i)
+                for t in range(T):
+                    sum_squares(i + 1, t, all_heads)
+                if in_range(i + 3):
+                    regroup(i + 3, 0, nc.scalar)
+                reciprocal_rms(i + 1, both_tiles)
+                if in_range(i + 3):
+                    regroup(i + 3, 1, nc.scalar)
+                for t in range(T):
+                    finish_v(i + 1, t)
+            if in_range(i + 4):
+                for t in range(T):
+                    transpose_tile(i + 4, t)
+            if in_range(i + 1):
+                if i > 0:
+                    rotate_cos(i, slice(2, 3))
+                    rotate_cos(i, slice(0, 2))
+                    rotate_sin(i, rotated_heads)
+                bring_tables(i + 1)
+                if in_range(i + 3) and i > 0:
+                    quantise(i + 3, both_tiles)
+                join(i, nc.gpsimd, rotated_heads, both_tiles)
                 store_k(i)
-        join_and_finish_last(ROUNDS - 1)
+                nc.sync.dma_start(out=q_view[:, :, tiles_of(i), :], in_=work_of[i][2][:, 0:2])
+
+        last = ROUNDS - 1
+        for h in (2, 0, 1):
+            heads = slice(h, h + 1)
+            rotate_cos(last, heads)
+            rotate_sin(last, heads)
+            if h == 2:
+                join(last, nc.gpsimd, heads, both_tiles)
+                store_k(last)
+        for h in (0, 1):
+            heads = slice(h, h + 1)
+            if h == 0:
+                join(last, nc.vector, heads, both_tiles)
+                nc.sync.dma_start(out=q_view[:, 0, tiles_of(last), :], in_=work_of[last][2][:, 0])
+            else:
+                for t in range(T):
+                    join(last, nc.vector, heads, slice(t, t + 1))
+                    nc.sync.dma_start(out=q_view[:, 1, last * T + t, :], in_=work_of[last][2][:, 1, t])

@@ -168,7 +168,7 @@ def tile_refattention_pa_t_kernel(
         gains = consts.tile([P, 2, D], BF16)
 
         def spread_gains():
-            bank = psum_table.tile([P, 4, D], F32)
+            bank = psum_table.tile([P, 4, D], F32, tag="bank")
             nc.tensor.matmul(
                 out=bank[:, 0:2, :].rearrange("p a d -> p (a d)"),
                 lhsT=ones[:],
@@ -275,7 +275,7 @@ def tile_refattention_pa_t_kernel(
                 nc.sync.dma_start(out=v_view[:, tiles_of(r), :], in_=v_of[r][:])
 
         def bring_tables(r):
-            bank = psum_table.tile([P, 4, D], F32)
+            bank = psum_table.tile([P, 4, D], F32, tag="bank")
             table_of[r] = bank
             for out, sign, rows in (
                 (bank[:, 0:2, :], plus_identity, tables[:, 0, tiles_of(r), :]),
@@ -343,23 +343,34 @@ def tile_refattention_pa_t_kernel(
         def store_k(r):
             nc.sync.dma_start(out=k_view[:, tiles_of(r), :], in_=work_of[r][2][:, 2])
 
-        warm = psum_prod.tile([P, HEADS, D], F32, tag="product")
-        for n in range(16):
-            nc.tensor.matmul(out=warm[:, n % HEADS, :], lhsT=ones[:], rhs=ones[:], start=True, stop=True)
+        warm = psum_table.tile([P, 4, D], F32, tag="bank")
+
+        def keep_warm(columns):
+            nc.tensor.matmul(
+                out=warm[:, 0, 0:columns], lhsT=identity[:], rhs=identity[:, 0:columns], start=True, stop=True
+            )
+
+        for n in range(5):
+            keep_warm(P)
         S, V = nc.scalar, nc.vector
         transpose_tile(0, 0)
+        keep_warm(P)
         regroup(0, 0, S)
         quantise(0, slice(0, 1))
         turn_head(0)
+        keep_warm(P)
         regroup_head(0, S)
         turn_head(1)
+        keep_warm(P)
         regroup_head(1, V)
         quantise_head(0)
         quantise_head(1)
         turn_head(2)
+        keep_warm(P)
         regroup_head(2, S)
         quantise_head(2)
         turn_head(3)
+        keep_warm(P)
         regroup_head(3, S)
         quantise_head(3)
         project(0, 0, slice(0, 2))

@@ -278,9 +278,9 @@ def tile_refattention_pa_t_kernel(
             bank = psum_table.tile([P, 4, D], F32, tag="bank")
             table_of[r] = bank
             for out, sign, rows in (
-                (bank[:, 0:2, :], plus_identity, tables[:, 0, tiles_of(r), :]),
-                (bank[:, 2, :].rearrange("p (t d) -> p t d", t=T), minus_identity, tables[:, 1, tiles_of(r), low]),
-                (bank[:, 3, :].rearrange("p (t d) -> p t d", t=T), plus_identity, tables[:, 1, tiles_of(r), high]),
+                (bank[:, T:, low], minus_identity, tables[:, 1, tiles_of(r), low]),
+                (bank[:, T:, high], plus_identity, tables[:, 1, tiles_of(r), high]),
+                (bank[:, 0:T, :], plus_identity, tables[:, 0, tiles_of(r), :]),
             ):
                 nc.tensor.matmul(out=out, lhsT=sign[:], rhs=rows, start=True, stop=True)
 
@@ -321,13 +321,12 @@ def tile_refattention_pa_t_kernel(
         def rotate_sin(r, heads):
             with_cos, with_sin, rotated = parts_of(r)
             n = heads.stop - heads.start
-            for a, half, other in ((2, low, high), (3, high, low)):
-                half_table = table_of[r][:, a, :].rearrange("p (t d) -> p t d", t=T)
-                times(
-                    with_sin[:, heads, :, half],
-                    gained_of[r][:, heads, :, other],
-                    half_table.unsqueeze(1).to_broadcast([P, n, T, HALF]),
-                )
+            halves = "p h t (a d) -> p h t a d"
+            times(
+                with_sin[:, heads].rearrange(halves, a=2),
+                gained_of[r][:, heads].rearrange(halves, a=2)[:, :, :, ::-1, :],
+                table_of[r][:, T:, :].unsqueeze(1).to_broadcast([P, n, T, D]).rearrange(halves, a=2),
+            )
 
         rotated_heads = slice(0, ROTATED)
 

@@ -343,10 +343,11 @@ def tile_refattention_pa_t_kernel(
             nc.sync.dma_start(out=k_view[:, tiles_of(r), :], in_=work_of[r][2][:, 2])
 
         warm = psum_table.tile([P, 4, D], F32, tag="bank")
+        warm_bank = [warm]
 
         def keep_warm(columns):
             nc.tensor.matmul(
-                out=warm[:, 0, 0:columns], lhsT=identity[:], rhs=identity[:, 0:columns], start=True, stop=True
+                out=warm_bank[0][:, 0, 0:columns], lhsT=identity[:], rhs=identity[:, 0:columns], start=True, stop=True
             )
 
         for n in range(5):
@@ -395,6 +396,10 @@ def tile_refattention_pa_t_kernel(
         transpose_tile(2, 0)
         regroup(2, 0, S)
         transpose_tile(2, 1)
+        warm = psum_turn.tile([P, TURNS, P], F32, tag="turned")
+        warm_bank[0] = warm
+        for n in range(1):
+            keep_warm(P)
         project(1, 0, all_heads)
         project(1, 1, all_heads)
         regroup(2, 1, S)
@@ -423,7 +428,7 @@ def tile_refattention_pa_t_kernel(
                 for t in range(T):
                     sum_squares(i + 1, t, all_heads)
                 if in_range(i + 3):
-                    regroup(i + 3, 0, nc.scalar)
+                    regroup(i + 3, 0, nc.vector if i == 0 else nc.scalar)
                 reciprocal_rms(i + 1, both_tiles)
                 if in_range(i + 3):
                     regroup(i + 3, 1, nc.scalar)
@@ -440,6 +445,8 @@ def tile_refattention_pa_t_kernel(
                 bring_tables(i + 1)
                 if in_range(i + 3) and i > 0:
                     quantise(i + 3, both_tiles)
+                if i in (1, 2):
+                    nc.vector.memset(parts_of(i)[2][:, 0, 0, 0:1], 0.0)
                 join(i, nc.gpsimd, rotated_heads, both_tiles)
                 store_k(i)
                 nc.sync.dma_start(out=q_view[:, :, tiles_of(i), :], in_=work_of[i][2][:, 0:2])

from contextlib import ExitStack

import concourse.mybir as mybir
from concourse.masks import make_identity

BF16 = mybir.dt.bfloat16
F32 = mybir.dt.float32
U32 = mybir.dt.uint32
U8 = mybir.dt.uint8
FP8X4 = mybir.dt.float8_e4m3fn_x4
ACT = mybir.ActivationFunctionType
ALU = mybir.AluOpType

P = 128
PACK = 4
K_PASS = P * PACK

TOKENS = 4096
HID = 1024
D = 128
HALF = D // 2
EPS = 1e-6
HEADS = 4
ROTATED = 3
V_HEAD = 3
FEATURES = HEADS * D

PASSES = HID // K_PASS
WORDS = HID // 2
TURNS = WORDS // P
TILES = TOKENS // P
T = 2
ROUNDS = TILES // T
LOAD_AHEAD = 7
TABLE_SPLITS = (4, 12)

FLOPS = 2 * TOKENS * HID * FEATURES


def tile_refattention_pa_t_kernel(
    tc, hidden_states, cos, sin, Wq, Wk, Wv, q_norm_w, k_norm_w, out_0, out_1, out_2
):
    nc = tc.nc

    x_view = hidden_states.flatten_outer_dims().rearrange("(p j) k -> p j k", j=TILES)
    cos_view = cos.flatten_outer_dims().rearrange("(p j) d -> p j d", j=TILES)
    sin_view = sin.flatten_outer_dims().rearrange("(p j) d -> p j d", j=TILES)
    q_view = out_0.flatten_outer_dims().rearrange("(h p j) d -> p h j d", h=2, j=TILES)
    k_view = out_1.flatten_outer_dims().rearrange("(p j) d -> p j d", j=TILES)
    v_view = out_2.flatten_outer_dims().rearrange("(p j) d -> p j d", j=TILES)

    with ExitStack() as stack:
        stack.enter_context(tc.manual_schedule())
        consts = stack.enter_context(tc.tile_pool(name="consts", bufs=1))
        x_pool = stack.enter_context(tc.tile_pool(name="x", bufs=ROUNDS))
        w_pool = stack.enter_context(tc.tile_pool(name="w", bufs=HEADS))
        stage = stack.enter_context(tc.tile_pool(name="stage", bufs=3))
        stats = stack.enter_context(tc.tile_pool(name="stats", bufs=3))
        work = stack.enter_context(tc.tile_pool(name="work", bufs=3))
        psum_turn = stack.enter_context(tc.psum_pool(name="psum_turn", bufs=3))
        psum_prod = stack.enter_context(tc.psum_pool(name="psum_prod", bufs=4))
        psum_table = stack.enter_context(tc.psum_pool(name="psum_table", bufs=1))

        identity = consts.tile([P, P], F32)
        make_identity(nc, identity[:])

        gain_rows = consts.tile([P, 2, D], BF16)
        nc.vector.memset(gain_rows[:], 0.0)

        w_raw = consts.tile([P, HEADS, HID], BF16)
        w_rows = (Wq[0:D, :], Wq[D : 2 * D, :], Wk, Wv)

        def load_head(h):
            nc.sync.dma_start(out=w_raw[:, h, :], in_=w_rows[h])

        x_of = {}

        def load_tokens(r, tiles):
            if r not in x_of:
                x_sb = x_pool.tile([P, T, HID], BF16)
                x_of[r] = x_sb
            first = r * T
            nc.sync.dma_start(
                out=x_of[r][:, tiles, :], in_=x_view[:, first + tiles.start : first + tiles.stop, :]
            )

        tables = consts.tile([P, 2, TILES, D], BF16)

        def load_tables(first, last):
            for a, view in enumerate((cos_view, sin_view)):
                nc.sync.dma_start(out=tables[:, a, first:last, :], in_=view[:, first:last, :])

        both_tiles = slice(0, T)
        load_tokens(0, slice(0, 1))
        load_head(0)
        load_head(1)
        for a, w in enumerate((q_norm_w, k_norm_w)):
            nc.sync.dma_start(out=gain_rows[0:1, a, :], in_=w.rearrange("(o d) -> o d", o=1))
        load_head(2)
        load_head(3)
        load_tokens(0, slice(1, 2))
        load_tokens(1, slice(0, 1))
        load_tokens(1, slice(1, 2))
        load_tables(0, TABLE_SPLITS[0])
        load_tokens(2, both_tiles)
        load_tokens(3, both_tiles)
        load_tables(TABLE_SPLITS[0], TABLE_SPLITS[1])
        load_tokens(4, both_tiles)
        load_tokens(5, both_tiles)
        load_tables(TABLE_SPLITS[1], TILES)
        load_tokens(6, both_tiles)

        ones = consts.tile([P, P], BF16)
        nc.vector.memset(ones[:], 1.0)
        eps = consts.tile([P, 1], F32)
        nc.vector.memset(eps[:], EPS)
        table_warmer = consts.tile([P, 1], F32)
        nc.scalar.activation(out=table_warmer[:], in_=eps[:], func=ACT.Abs_reciprocal_sqrt)
        plus_identity = consts.tile([P, P], BF16)
        minus_identity = consts.tile([P, P], BF16)
        nc.vector.tensor_copy(out=plus_identity[:], in_=identity[:])
        nc.vector.tensor_scalar(
            out=minus_identity[:], in0=identity[:], scalar1=-1.0, scalar2=None, op0=ALU.mult
        )

        def turn(turned, rows_as_words):
            for c in range(TURNS):
                g, u = divmod(c, 2)
                every_second = rows_as_words[:, 2 * P * g + u : 2 * P * (g + 1) : 2]
                nc.tensor.transpose(turned[:, c, :], every_second, identity[:])

        def side_by_side(turned):
            return turned[:].rearrange("p (g u) r -> p g r u", u=2)

        def copy_on(engine, out, in_):
            if engine is nc.scalar:
                nc.scalar.copy(out=out, in_=in_)
            else:
                nc.vector.tensor_copy(out=out, in_=in_)

        w_words = w_raw[:].bitcast(F32)
        w_codes = consts.tile([P, PASSES, FEATURES], U32, align_bytes=64)
        w_scales = consts.tile([P, PASSES, FEATURES], U8, align_bytes=64)
        w_turned_of = {}
        w_grouped_of = {}

        def turn_head(h):
            turned = psum_prod.tile([P, TURNS, P], F32, tag="product")
            turn(turned, w_words[:, h, :])
            w_turned_of[h] = turned

        def regroup_head(h, engine):
            w_grouped = w_pool.tile([P, PASSES, D, PACK], BF16, align_bytes=64)
            w_grouped_of[h] = w_grouped
            copy_on(engine, w_grouped[:].bitcast(F32), side_by_side(w_turned_of[h]))

        def quantise_head(h):
            columns = slice(h * D, (h + 1) * D)
            for g in range(PASSES):
                nc.vector.quantize_mx(
                    out=w_codes[:, g, columns].bitcast(FP8X4),
                    scales=w_scales[:, g, columns],
                    in_=w_grouped_of[h][:, g, :, :].rearrange("p f t -> p (f t)"),
                )

        low = slice(0, HALF)
        high = slice(HALF, D)
        gains = consts.tile([P, 2, D], BF16)

        def spread_gains():
            bank = psum_table.tile([P, 4, D], F32, tag="bank")
            nc.tensor.matmul(
                out=bank[:, 0:2, :].rearrange("p a d -> p (a d)"),
                lhsT=ones[:],
                rhs=gain_rows[:].rearrange("p a d -> p (a d)"),
                start=True,
                stop=True,
            )
            nc.scalar.copy(out=gains[:], in_=bank[:, 0:2, :])

        turned_of = {}
        grouped_of = {}
        codes_of = {}
        product_of = {}
        sums_of = {}
        rstd_of = {}
        table_of = {}
        gained_of = {}
        work_of = {}
        v_of = {}

        def tiles_of(r):
            return slice(r * T, (r + 1) * T)

        def transpose_tile(r, t):
            turned = psum_turn.tile([P, TURNS, P], F32)
            turn(turned, x_of[r][:].bitcast(F32)[:, t, :])
            turned_of[r, t] = turned

        def regroup(r, t, engine):
            if r not in grouped_of:
                grouped = stage.tile([P, T, PASSES, P, PACK], BF16, align_bytes=64)
                grouped_of[r] = grouped
            words = grouped_of[r][:].bitcast(F32)
            copy_on(engine, words[:, t], side_by_side(turned_of[r, t]))

        def quantise(r, span):
            if r not in codes_of:
                codes = stage.tile([P, T, PASSES, P], U32, align_bytes=64)
                scales = stage.tile([P, T, PASSES, P], U8, align_bytes=64)
                codes_of[r] = (codes, scales)
            codes, scales = codes_of[r]
            nc.vector.quantize_mx(
                out=codes[:, span].rearrange("p t g r -> p (t g r)").bitcast(FP8X4),
                scales=scales[:, span].rearrange("p t g r -> p (t g r)"),
                in_=grouped_of[r][:, span].rearrange("p t g r v -> p (t g r v)"),
            )

        def project(r, t, heads):
            codes, scales = codes_of[r]
            if (r, t) not in product_of:
                product = psum_prod.tile([P, HEADS, D], F32, tag="product")
                product_of[r, t] = product
            columns = slice(heads.start * D, heads.stop * D)
            for g in range(PASSES):
                nc.tensor.matmul_mx(
                    out=product_of[r, t][:, heads, :].rearrange("p h d -> p (h d)"),
                    lhsT=codes[:, t, g, :].bitcast(FP8X4),
                    lhsT_scale=scales[:, t, g, :],
                    rhs=w_codes[:, g, columns].bitcast(FP8X4),
                    rhs_scale=w_scales[:, g, columns],
                    start=(g == 0),
                    stop=(g == PASSES - 1),
                )

        all_heads = slice(0, HEADS)

        def sum_squares(r, t, heads):
            if r not in sums_of:
                sums = stats.tile([P, T, HEADS], F32)
                squares = stats.tile([P, T, HEADS, D], BF16)
                sums_of[r] = (sums, squares)
            sums, squares = sums_of[r]
            for h in range(heads.start, heads.stop):
                nc.scalar.activation(
                    out=squares[:, t, h, :],
                    in_=product_of[r, t][:, h, :],
                    func=ACT.Square,
                    accum_out=sums[:, t, h : h + 1],
                )

        def reciprocal_rms(r, span):
            if r not in rstd_of:
                rstd = stats.tile([P, T, HEADS], F32)
                rstd_of[r] = rstd
            nc.scalar.activation(
                out=rstd_of[r][:, span, :],
                in_=sums_of[r][0][:, span, :],
                func=ACT.Abs_reciprocal_sqrt,
                scale=1.0 / D,
                bias=eps[:],
            )

        def finish_v(r, t):
            if r not in v_of:
                v_out = stats.tile([P, T, D], F32)
                v_of[r] = v_out
            nc.scalar.activation(
                out=v_of[r][:, t, :],
                in_=product_of[r, t][:, V_HEAD, :],
                func=ACT.Copy,
                scale=rstd_of[r][:, t, V_HEAD : V_HEAD + 1],
            )
            if t == T - 1:
                nc.sync.dma_start(out=v_view[:, tiles_of(r), :], in_=v_of[r][:])

        def bring_tables(r):
            bank = psum_table.tile([P, 4, D], F32, tag="bank")
            table_of[r] = bank
            for out, sign, rows in (
                (bank[:, T:, low], minus_identity, tables[:, 1, tiles_of(r), low]),
                (bank[:, T:, high], plus_identity, tables[:, 1, tiles_of(r), high]),
                (bank[:, 0:T, :], plus_identity, tables[:, 0, tiles_of(r), :]),
            ):
                nc.tensor.matmul(out=out, lhsT=sign[:], rhs=rows, start=True, stop=True)

        def gain(r, t):
            if r not in gained_of:
                gained = work.tile([P, ROTATED, T, D], F32)
                gained_of[r] = gained
            for h in ((0, 1, 2) if t == 0 else (2, 0, 1)):
                nc.vector.scalar_tensor_tensor(
                    out=gained_of[r][:, h, t, :],
                    in0=product_of[r, t][:, h, :],
                    scalar=rstd_of[r][:, t, h : h + 1],
                    in1=gains[:, h // 2, :],
                    op0=ALU.mult,
                    op1=ALU.mult,
                )

        def times(out, in0, in1):
            nc.vector.tensor_tensor(out=out, in0=in0, in1=in1, op=ALU.mult)

        def parts_of(r):
            if r not in work_of:
                with_cos = work.tile([P, ROTATED, T, D], F32)
                with_sin = work.tile([P, ROTATED, T, D], F32)
                rotated = work.tile([P, ROTATED, T, D], F32)
                work_of[r] = (with_cos, with_sin, rotated)
            return work_of[r]

        def rotate_cos(r, heads):
            with_cos, with_sin, rotated = parts_of(r)
            n = heads.stop - heads.start
            times(
                with_cos[:, heads],
                gained_of[r][:, heads],
                table_of[r][:, 0:2, :].unsqueeze(1).to_broadcast([P, n, T, D]),
            )

        def rotate_sin(r, heads):
            with_cos, with_sin, rotated = parts_of(r)
            n = heads.stop - heads.start
            halves = "p h t (a d) -> p h t a d"
            times(
                with_sin[:, heads].rearrange(halves, a=2),
                gained_of[r][:, heads].rearrange(halves, a=2)[:, :, :, ::-1, :],
                table_of[r][:, T:, :].unsqueeze(1).to_broadcast([P, n, T, D]).rearrange(halves, a=2),
            )

        rotated_heads = slice(0, ROTATED)

        def join(r, engine, heads, span):
            with_cos, with_sin, rotated = parts_of(r)
            engine.tensor_tensor(
                out=rotated[:, heads, span],
                in0=with_cos[:, heads, span],
                in1=with_sin[:, heads, span],
                op=ALU.add,
            )

        def store_k(r):
            nc.sync.dma_start(out=k_view[:, tiles_of(r), :], in_=work_of[r][2][:, 2])

        warm = psum_table.tile([P, 4, D], F32, tag="bank")
        warm_bank = [warm]

        def keep_warm(columns):
            nc.tensor.matmul(
                out=warm_bank[0][:, 0, 0:columns], lhsT=identity[:], rhs=identity[:, 0:columns], start=True, stop=True
            )

        for n in range(5):
            keep_warm(P)
        S, V = nc.scalar, nc.vector
        transpose_tile(0, 0)
        keep_warm(P)
        regroup(0, 0, S)
        quantise(0, slice(0, 1))
        turn_head(0)
        keep_warm(P)
        regroup_head(0, S)
        turn_head(1)
        keep_warm(P)
        regroup_head(1, V)
        quantise_head(0)
        quantise_head(1)
        turn_head(2)
        keep_warm(P)
        regroup_head(2, S)
        quantise_head(2)
        turn_head(3)
        keep_warm(P)
        regroup_head(3, S)
        quantise_head(3)
        project(0, 0, slice(0, 2))
        sum_squares(0, 0, slice(0, 2))
        transpose_tile(0, 1)
        regroup(0, 1, V)
        spread_gains()
        project(0, 0, slice(2, 4))
        sum_squares(0, 0, slice(2, 4))
        quantise(0, slice(1, 2))
        reciprocal_rms(0, slice(0, 1))
        transpose_tile(1, 0)
        project(0, 1, all_heads)
        bring_tables(0)
        gain(0, 0)
        transpose_tile(1, 1)
        regroup(1, 0, V)
        sum_squares(0, 1, all_heads)
        reciprocal_rms(0, slice(1, 2))
        regroup(1, 1, S)
        gain(0, 1)
        quantise(1, both_tiles)
        transpose_tile(2, 0)
        regroup(2, 0, S)
        transpose_tile(2, 1)
        warm = psum_turn.tile([P, TURNS, P], F32, tag="turned")
        warm_bank[0] = warm
        for n in range(1):
            keep_warm(P)
        project(1, 0, all_heads)
        project(1, 1, all_heads)
        regroup(2, 1, S)
        for t in range(T):
            finish_v(0, t)
            transpose_tile(3, t)
        rotate_cos(0, rotated_heads)
        rotate_sin(0, rotated_heads)
        quantise(2, both_tiles)

        def in_range(r):
            return r < ROUNDS

        for i in range(ROUNDS):
            if in_range(i + LOAD_AHEAD):
                load_tokens(i + LOAD_AHEAD, both_tiles)
            if i > 0:
                for t in range(T):
                    gain(i, t)
            if i == 1:
                quantise(3, both_tiles)
            if in_range(i + 2):
                for t in range(T):
                    project(i + 2, t, all_heads)
            if in_range(i + 1):
                for t in range(T):
                    sum_squares(i + 1, t, all_heads)
                if in_range(i + 3):
                    regroup(i + 3, 0, nc.vector if i == 0 else nc.scalar)
                reciprocal_rms(i + 1, both_tiles)
                if in_range(i + 3):
                    regroup(i + 3, 1, nc.scalar)
                for t in range(T):
                    finish_v(i + 1, t)
            if in_range(i + 4):
                for t in range(T):
                    transpose_tile(i + 4, t)
            if in_range(i + 1):
                if i > 0:
                    rotate_cos(i, slice(2, 3))
                    rotate_cos(i, slice(0, 2))
                    rotate_sin(i, rotated_heads)
                bring_tables(i + 1)
                if in_range(i + 3) and i > 0:
                    quantise(i + 3, both_tiles)
                if i in (1, 2):
                    nc.vector.memset(parts_of(i)[2][:, 0, 0, 0:1], 0.0)
                join(i, nc.gpsimd, rotated_heads, both_tiles)
                store_k(i)
                nc.sync.dma_start(out=q_view[:, :, tiles_of(i), :], in_=work_of[i][2][:, 0:2])

        last = ROUNDS - 1
        for h in (2, 0, 1):
            heads = slice(h, h + 1)
            rotate_cos(last, heads)
            rotate_sin(last, heads)
            if h == 2:
                join(last, nc.gpsimd, heads, both_tiles)
                store_k(last)
        for h in (0, 1):
            heads = slice(h, h + 1)
            if h == 0:
                join(last, nc.vector, heads, both_tiles)
                nc.sync.dma_start(out=q_view[:, 0, tiles_of(last), :], in_=work_of[last][2][:, 0])
            else:
                for t in range(T):
                    join(last, nc.vector, heads, slice(t, t + 1))
                    nc.sync.dma_start(out=q_view[:, 1, last * T + t, :], in_=work_of[last][2][:, 1, t])
